import numpy as np
import ml_dtypes


def mxq(x, axis, fmt="e4m3"):
    dtype, down = {"e4m3": (ml_dtypes.float8_e4m3fn, 7), "e5m2": (ml_dtypes.float8_e5m2, 14)}[fmt]
    v = np.moveaxis(np.asarray(x, np.float32).astype(ml_dtypes.bfloat16).astype(np.float64), axis, -1)
    blocks = v.reshape(v.shape[:-1] + (-1, 32))
    amax = np.abs(blocks).max(-1, keepdims=True)
    byte = np.maximum(np.where(amax > 0, np.frexp(amax)[1] - 1 + 127, 0) - down, 1)
    scale = np.exp2(byte - 127.0)
    codes = (blocks / scale).astype(np.float32).astype(dtype).astype(np.float64)
    return np.moveaxis((codes * scale).reshape(v.shape), -1, axis)


WIDE = False


def mx_kscale(k):
    if not WIDE:
        return np.ones(k)
    levels = np.array([10, -10, 5, -5, 0])
    a = np.random.permutation(np.resize(levels, k // 512 * 4)).reshape(k // 512, 4)
    idx = np.arange(k)
    return np.exp2(a[idx // 512, idx % 128 // 32])


BF16 = ml_dtypes.bfloat16


def bf(x):
    return np.asarray(x, np.float32).astype(BF16)


def f64(x):
    return np.asarray(x).astype(np.float64)


B, NH, T, D, N = 1, 1, 512, 256, 8192
THETA = 2.0 ** 16
SCALE = N ** -0.5


def rope_tables():
    pair = np.repeat(np.arange(N // 2), 2)
    freqs = 1.0 / THETA ** (pair * 2.0 / N)
    angles = np.arange(T)[:, None] * freqs[None, :]
    return np.cos(angles), np.sin(angles)


def rope(v, cos, sin):
    v_rot = np.stack([-v[..., 1::2], v[..., ::2]], axis=-1).reshape(v.shape)
    return v * cos + v_rot * sin


def setup_inputs():
    u = mx_kscale(T)
    cos, sin = rope_tables()
    return {"Q": bf(np.random.uniform(size=(B, NH, T, N)) * 1.2 / N ** 0.25 * u[:, None]),
            "V": bf(np.random.standard_normal((B, 1, T, D)) * 45.0 / np.sqrt(T) / u[:, None]),
            "state": bf(np.random.standard_normal((B, NH, N, D)) * 60.0 / N ** 0.75),
            "cos": bf(cos), "sin": bf(sin)}


def reference(Q, V, state, cos, sin):
    QR = rope(f64(Q), f64(cos), f64(sin))
    chunk_state = (np.swapaxes(mxq(QR, 2, "e4m3"), -2, -1) @ mxq(f64(V), 2, "e4m3")) * SCALE
    return f64(state) + chunk_state

@@ -1,0 +1,144 @@
+from contextlib import ExitStack
+
+import concourse.mybir as mybir
+
+F32 = mybir.dt.float32
+BF16 = mybir.dt.bfloat16
+U32 = mybir.dt.uint32
+U8 = mybir.dt.uint8
+FP8X4 = mybir.dt.float8_e4m3fn_x4
+MULT = mybir.AluOpType.mult
+ADD = mybir.AluOpType.add
+SUBTRACT = mybir.AluOpType.subtract
+
+P = 128
+PACK = 4
+TOKENS = P * PACK
+FEATURES = 8192
+VALUES = 256
+SCALE = FEATURES**-0.5
+
+CHUNK = 1024
+CHUNKS = FEATURES // CHUNK
+HALF = CHUNK // 2
+GROUP = 2 * P
+GROUPS = CHUNK // GROUP
+
+FLOPS = 2 * TOKENS * FEATURES * VALUES
+
+
+def rope_half(nc, products, q_same, q_other, cos_half, sin_half, combine, rotated):
+    same = products.tile([P, PACK, HALF], F32)
+    nc.vector.tensor_tensor(out=same[:], in0=q_same, in1=cos_half, op=MULT)
+    other = products.tile([P, PACK, HALF], F32)
+    nc.vector.tensor_tensor(out=other[:], in0=q_other, in1=sin_half, op=MULT)
+    nc.vector.tensor_tensor(
+        out=rotated,
+        in0=same[:].rearrange("p j i -> p i j"),
+        in1=other[:].rearrange("p j i -> p i j"),
+        op=combine,
+    )
+
+
+def add_to_state(nc, results, sums, old_state, out_rows):
+    new_state = results.tile([P, GROUPS, 2 * VALUES], F32)
+    for g in range(GROUPS):
+        nc.vector.scalar_tensor_tensor(
+            out=new_state[:, g, :],
+            in0=sums[g][:].rearrange("m e d -> m (e d)"),
+            scalar=SCALE,
+            in1=old_state[:, g, :],
+            op0=MULT,
+            op1=ADD,
+        )
+    nc.scalar.dma_start(out=out_rows, in_=new_state[:])
+
+
+def tile_attention_pb_kernel(tc, Q, V, state, cos, sin, out):
+    nc = tc.nc
+
+    q_rows = Q.flatten_outer_dims().rearrange("(p j) f -> p j f", j=PACK)
+    cos_rows = cos.rearrange("(p j) f -> p j f", j=PACK)
+    sin_rows = sin.rearrange("(p j) f -> p j f", j=PACK)
+    v_rows = V.flatten_outer_dims().rearrange("(p j) d -> p j d", j=PACK)
+    state_rows = state.flatten_outer_dims().rearrange("(n m e) d -> m n (e d)", m=P, e=2)
+    out_rows = out.flatten_outer_dims().rearrange("(n m e) d -> m n (e d)", m=P, e=2)
+
+    with ExitStack() as ctx:
+        keep = ctx.enter_context(tc.tile_pool(name="keep", bufs=1))
+        loads = ctx.enter_context(tc.tile_pool(name="loads", bufs=3))
+        products = ctx.enter_context(tc.tile_pool(name="products", bufs=2))
+        quantised = ctx.enter_context(tc.tile_pool(name="quantised", bufs=2))
+        results = ctx.enter_context(tc.tile_pool(name="results", bufs=2))
+        psum = ctx.enter_context(tc.psum_pool(name="psum", bufs=2 * GROUPS))
+
+        v_raw = keep.tile([P, PACK, VALUES], BF16)
+        nc.sync.dma_start(out=v_raw[:], in_=v_rows)
+        v_grouped = keep.tile([P, VALUES, PACK], BF16, align_bytes=64)
+        nc.vector.tensor_copy(out=v_grouped[:], in_=v_raw[:].rearrange("p j d -> p d j"))
+        v_codes = keep.tile([P, VALUES], U32, align_bytes=64)
+        v_scales = keep.tile([P, VALUES], U8, align_bytes=64)
+        nc.vector.quantize_mx(
+            out=v_codes[:].bitcast(FP8X4),
+            scales=v_scales[:],
+            in_=v_grouped[:].rearrange("p d j -> p (d j)"),
+        )
+
+        waiting = None
+        for c in range(CHUNKS):
+            features = slice(c * CHUNK, (c + 1) * CHUNK)
+            groups = slice(c * GROUPS, (c + 1) * GROUPS)
+
+            q_sb = loads.tile([P, PACK, CHUNK], BF16)
+            nc.sync.dma_start(out=q_sb[:], in_=q_rows[:, :, features])
+            cos_sb = loads.tile([P, PACK, CHUNK], BF16)
+            nc.sync.dma_start(out=cos_sb[:], in_=cos_rows[:, :, features])
+            sin_sb = loads.tile([P, PACK, CHUNK], BF16)
+            nc.sync.dma_start(out=sin_sb[:], in_=sin_rows[:, :, features])
+            old_state = loads.tile([P, GROUPS, 2 * VALUES], BF16)
+            nc.sync.dma_start(out=old_state[:], in_=state_rows[:, groups, :])
+
+            q_halves = q_sb[:].rearrange("p j (i e) -> p e j i", e=2)
+            cos_halves = cos_sb[:].rearrange("p j (i e) -> p e j i", e=2)
+            sin_halves = sin_sb[:].rearrange("p j (i e) -> p e j i", e=2)
+
+            rotated = quantised.tile([P, 2, HALF, PACK], BF16, align_bytes=64)
+            rope_half(
+                nc, products, q_halves[:, 0], q_halves[:, 1], cos_halves[:, 0], sin_halves[:, 0],
+                SUBTRACT, rotated[:, 0],
+            )
+            rope_half(
+                nc, products, q_halves[:, 1], q_halves[:, 0], cos_halves[:, 1], sin_halves[:, 1],
+                ADD, rotated[:, 1],
+            )
+
+            if waiting is not None:
+                add_to_state(nc, results, *waiting)
+
+            codes = quantised.tile([P, 2, HALF], U32, align_bytes=64)
+            scales = quantised.tile([P, 2, HALF], U8, align_bytes=64)
+            for e in range(2):
+                nc.vector.quantize_mx(
+                    out=codes[:, e, :].bitcast(FP8X4),
+                    scales=scales[:, e, :],
+                    in_=rotated[:, e].rearrange("p i j -> p (i j)"),
+                )
+
+            sums = []
+            for g in range(GROUPS):
+                pairs = slice(g * P, (g + 1) * P)
+                acc = psum.tile([P, 2, VALUES], F32)
+                for e in range(2):
+                    nc.tensor.matmul_mx(
+                        out=acc[:, e, :],
+                        lhsT=codes[:, e, pairs].bitcast(FP8X4),
+                        lhsT_scale=scales[:, e, pairs],
+                        rhs=v_codes[:].bitcast(FP8X4),
+                        rhs_scale=v_scales[:],
+                        start=True,
+                        stop=True,
+                    )
+                sums.append(acc)
+            waiting = (sums, old_state, out_rows[:, groups, :])
+
+        add_to_state(nc, results, *waiting)

@@ -1,6 +1,7 @@
 from contextlib import ExitStack
 
 import concourse.mybir as mybir
+from concourse.masks import make_identity
 
 F32 = mybir.dt.float32
 BF16 = mybir.dt.bfloat16
@@ -19,39 +20,69 @@ VALUES = 256
 SCALE = FEATURES**-0.5
 
 CHUNK = 1024
-CHUNKS = FEATURES // CHUNK
-HALF = CHUNK // 2
+PART = 512
+PARTS = FEATURES // PART
+PARTS_PER_CHUNK = CHUNK // PART
+HALF = PART // 2
 GROUP = 2 * P
-GROUPS = CHUNK // GROUP
+GROUPS = PART // GROUP
+BANK_TOKENS = 2
+BANKS = PACK // BANK_TOKENS
+SQUARES = PART // P
 
 FLOPS = 2 * TOKENS * FEATURES * VALUES
 
 
-def rope_half(nc, products, q_same, q_other, cos_half, sin_half, combine, rotated):
+def halves(rows):
+    return rows.rearrange("p j (i e) -> p e j i", e=2)
+
+
+def q_into_psum(nc, turned_psum, turned_sbuf, q_psum, identity, q_part):
+    turned_back = []
+    copies = []
+    for k in range(BANKS):
+        turned = turned_psum.tile([P, BANK_TOKENS, SQUARES, P], BF16)
+        for j in range(BANK_TOKENS):
+            for s in range(SQUARES):
+                nc.tensor.transpose(
+                    out=turned[:, j, s, :],
+                    in_=q_part[:, k * BANK_TOKENS + j, s * P : (s + 1) * P],
+                    identity=identity,
+                )
+        turned_copy = turned_sbuf.tile([P, BANK_TOKENS, SQUARES, P], BF16)
+        nc.scalar.copy(out=turned_copy[:], in_=turned[:])
+        copies.append(turned_copy)
+    for k in range(BANKS):
+        q_bank = q_psum.tile([P, BANK_TOKENS, PART], BF16)
+        for j in range(BANK_TOKENS):
+            for s in range(SQUARES):
+                nc.tensor.transpose(
+                    out=q_bank[:, j, s * P : (s + 1) * P],
+                    in_=copies[k][:, j, s, :],
+                    identity=identity,
+                )
+        turned_back.append(q_bank)
+    return turned_back
+
+
+def rope_half(nc, products, q_banks, cos_part, sin_part, e, combine, rotated):
     same = products.tile([P, PACK, HALF], F32)
-    nc.vector.tensor_tensor(out=same[:], in0=q_same, in1=cos_half, op=MULT)
     other = products.tile([P, PACK, HALF], F32)
-    nc.vector.tensor_tensor(out=other[:], in0=q_other, in1=sin_half, op=MULT)
-    nc.vector.tensor_tensor(
+    for k in range(BANKS):
+        tokens = slice(k * BANK_TOKENS, (k + 1) * BANK_TOKENS)
+        q_halves = halves(q_banks[k][:])
+        nc.vector.tensor_tensor(
+            out=same[:, tokens, :], in0=q_halves[:, e], in1=halves(cos_part[:, tokens, :])[:, e], op=MULT
+        )
+        nc.vector.tensor_tensor(
+            out=other[:, tokens, :], in0=q_halves[:, 1 - e], in1=halves(sin_part[:, tokens, :])[:, e], op=MULT
+        )
+    nc.gpsimd.tensor_tensor(
         out=rotated,
         in0=same[:].rearrange("p j i -> p i j"),
         in1=other[:].rearrange("p j i -> p i j"),
         op=combine,
     )
-
-
-def add_to_state(nc, results, sums, old_state, out_rows):
-    new_state = results.tile([P, GROUPS, 2 * VALUES], F32)
-    for g in range(GROUPS):
-        nc.vector.scalar_tensor_tensor(
-            out=new_state[:, g, :],
-            in0=sums[g][:].rearrange("m e d -> m (e d)"),
-            scalar=SCALE,
-            in1=old_state[:, g, :],
-            op0=MULT,
-            op1=ADD,
-        )
-    nc.scalar.dma_start(out=out_rows, in_=new_state[:])
 
 
 def tile_attention_pb_kernel(tc, Q, V, state, cos, sin, out):
@@ -67,10 +98,16 @@ def tile_attention_pb_kernel(tc, Q, V, state, cos, sin, out):
     with ExitStack() as ctx:
         keep = ctx.enter_context(tc.tile_pool(name="keep", bufs=1))
         loads = ctx.enter_context(tc.tile_pool(name="loads", bufs=3))
-        products = ctx.enter_context(tc.tile_pool(name="products", bufs=2))
-        quantised = ctx.enter_context(tc.tile_pool(name="quantised", bufs=2))
-        results = ctx.enter_context(tc.tile_pool(name="results", bufs=2))
-        psum = ctx.enter_context(tc.psum_pool(name="psum", bufs=2 * GROUPS))
+        turned_sbuf = ctx.enter_context(tc.tile_pool(name="turned_sbuf", bufs=2 * BANKS))
+        products = ctx.enter_context(tc.tile_pool(name="products", bufs=6))
+        quantised = ctx.enter_context(tc.tile_pool(name="quantised", bufs=3))
+        results = ctx.enter_context(tc.tile_pool(name="results", bufs=3))
+        turned_psum = ctx.enter_context(tc.psum_pool(name="turned_psum", bufs=BANKS))
+        q_psum = ctx.enter_context(tc.psum_pool(name="q_psum", bufs=2 * BANKS))
+        sums_psum = ctx.enter_context(tc.psum_pool(name="sums_psum", bufs=GROUPS))
+
+        identity = keep.tile([P, P], BF16)
+        make_identity(nc, identity[:])
 
         v_raw = keep.tile([P, PACK, VALUES], BF16)
         nc.sync.dma_start(out=v_raw[:], in_=v_rows)
@@ -84,61 +121,73 @@ def tile_attention_pb_kernel(tc, Q, V, state, cos, sin, out):
             in_=v_grouped[:].rearrange("p d j -> p (d j)"),
         )
 
-        waiting = None
-        for c in range(CHUNKS):
-            features = slice(c * CHUNK, (c + 1) * CHUNK)
-            groups = slice(c * GROUPS, (c + 1) * GROUPS)
+        q_part, cos_part, sin_part, state_part = {}, {}, {}, {}
+        q_banks, rotated, sums = {}, {}, {}
 
-            q_sb = loads.tile([P, PACK, CHUNK], BF16)
-            nc.sync.dma_start(out=q_sb[:], in_=q_rows[:, :, features])
-            cos_sb = loads.tile([P, PACK, CHUNK], BF16)
-            nc.sync.dma_start(out=cos_sb[:], in_=cos_rows[:, :, features])
-            sin_sb = loads.tile([P, PACK, CHUNK], BF16)
-            nc.sync.dma_start(out=sin_sb[:], in_=sin_rows[:, :, features])
-            old_state = loads.tile([P, GROUPS, 2 * VALUES], BF16)
-            nc.sync.dma_start(out=old_state[:], in_=state_rows[:, groups, :])
+        for turn in range(-1, PARTS + 2):
+            u = turn + 1
+            if u < PARTS:
+                if u % PARTS_PER_CHUNK == 0:
+                    c = u // PARTS_PER_CHUNK
+                    features = slice(c * CHUNK, (c + 1) * CHUNK)
+                    groups = slice(c * CHUNK // GROUP, (c + 1) * CHUNK // GROUP)
+                    q_sb = loads.tile([P, PACK, CHUNK], BF16)
+                    nc.sync.dma_start(out=q_sb[:], in_=q_rows[:, :, features])
+                    cos_sb = loads.tile([P, PACK, CHUNK], BF16)
+                    nc.sync.dma_start(out=cos_sb[:], in_=cos_rows[:, :, features])
+                    sin_sb = loads.tile([P, PACK, CHUNK], BF16)
+                    nc.sync.dma_start(out=sin_sb[:], in_=sin_rows[:, :, features])
+                    state_sb = loads.tile([P, CHUNK // GROUP, 2 * VALUES], BF16)
+                    nc.sync.dma_start(out=state_sb[:], in_=state_rows[:, groups, :])
+                    for h in range(PARTS_PER_CHUNK):
+                        q_part[u + h] = q_sb[:, :, h * PART : (h + 1) * PART]
+                        cos_part[u + h] = cos_sb[:, :, h * PART : (h + 1) * PART]
+                        sin_part[u + h] = sin_sb[:, :, h * PART : (h + 1) * PART]
+                        state_part[u + h] = state_sb[:, h * GROUPS : (h + 1) * GROUPS, :]
+                q_banks[u] = q_into_psum(nc, turned_psum, turned_sbuf, q_psum, identity[:], q_part[u])
 
-            q_halves = q_sb[:].rearrange("p j (i e) -> p e j i", e=2)
-            cos_halves = cos_sb[:].rearrange("p j (i e) -> p e j i", e=2)
-            sin_halves = sin_sb[:].rearrange("p j (i e) -> p e j i", e=2)
+            u = turn
+            if 0 <= u < PARTS:
+                rotated_u = quantised.tile([P, 2, HALF, PACK], BF16, align_bytes=64)
+                rope_half(nc, products, q_banks[u], cos_part[u], sin_part[u], 0, SUBTRACT, rotated_u[:, 0])
+                rope_half(nc, products, q_banks[u], cos_part[u], sin_part[u], 1, ADD, rotated_u[:, 1])
+                rotated[u] = rotated_u
 
-            rotated = quantised.tile([P, 2, HALF, PACK], BF16, align_bytes=64)
-            rope_half(
-                nc, products, q_halves[:, 0], q_halves[:, 1], cos_halves[:, 0], sin_halves[:, 0],
-                SUBTRACT, rotated[:, 0],
-            )
-            rope_half(
-                nc, products, q_halves[:, 1], q_halves[:, 0], cos_halves[:, 1], sin_halves[:, 1],
-                ADD, rotated[:, 1],
-            )
-
-            if waiting is not None:
-                add_to_state(nc, results, *waiting)
-
-            codes = quantised.tile([P, 2, HALF], U32, align_bytes=64)
-            scales = quantised.tile([P, 2, HALF], U8, align_bytes=64)
-            for e in range(2):
-                nc.vector.quantize_mx(
-                    out=codes[:, e, :].bitcast(FP8X4),
-                    scales=scales[:, e, :],
-                    in_=rotated[:, e].rearrange("p i j -> p (i j)"),
-                )
-
-            sums = []
-            for g in range(GROUPS):
-                pairs = slice(g * P, (g + 1) * P)
-                acc = psum.tile([P, 2, VALUES], F32)
-                for e in range(2):
-                    nc.tensor.matmul_mx(
-                        out=acc[:, e, :],
-                        lhsT=codes[:, e, pairs].bitcast(FP8X4),
-                        lhsT_scale=scales[:, e, pairs],
-                        rhs=v_codes[:].bitcast(FP8X4),
-                        rhs_scale=v_scales[:],
-                        start=True,
-                        stop=True,
+            u = turn - 2
+            if 0 <= u < PARTS:
+                new_state = results.tile([P, GROUPS, 2 * VALUES], F32)
+                for g in range(GROUPS):
+                    nc.vector.scalar_tensor_tensor(
+                        out=new_state[:, g, :],
+                        in0=sums[u][g][:].rearrange("m e d -> m (e d)"),
+                        scalar=SCALE,
+                        in1=state_part[u][:, g, :],
+                        op0=MULT,
+                        op1=ADD,
                     )
-                sums.append(acc)
-            waiting = (sums, old_state, out_rows[:, groups, :])
+                nc.scalar.dma_start(out=out_rows[:, u * GROUPS : (u + 1) * GROUPS, :], in_=new_state[:])
 
-        add_to_state(nc, results, *waiting)
+            u = turn - 1
+            if 0 <= u < PARTS:
+                codes = quantised.tile([P, 2, HALF], U32, align_bytes=64)
+                scales = quantised.tile([P, 2, HALF], U8, align_bytes=64)
+                nc.vector.quantize_mx(
+                    out=codes[:].rearrange("p e i -> p (e i)").bitcast(FP8X4),
+                    scales=scales[:].rearrange("p e i -> p (e i)"),
+                    in_=rotated[u][:].rearrange("p e i j -> p (e i j)"),
+                )
+                sums[u] = []
+                for g in range(GROUPS):
+                    pairs = slice(g * P, (g + 1) * P)
+                    acc = sums_psum.tile([P, 2, VALUES], F32)
+                    for e in range(2):
+                        nc.tensor.matmul_mx(
+                            out=acc[:, e, :],
+                            lhsT=codes[:, e, pairs].bitcast(FP8X4),
+                            lhsT_scale=scales[:, e, pairs],
+                            rhs=v_codes[:].bitcast(FP8X4),
+                            rhs_scale=v_scales[:],
+                            start=True,
+                            stop=True,
+                        )
+                    sums[u].append(acc)

@@ -72,10 +72,10 @@ def rope_half(nc, products, q_banks, cos_part, sin_part, e, combine, rotated):
         tokens = slice(k * BANK_TOKENS, (k + 1) * BANK_TOKENS)
         q_halves = halves(q_banks[k][:])
         nc.vector.tensor_tensor(
-            out=same[:, tokens, :], in0=q_halves[:, e], in1=halves(cos_part[:, tokens, :])[:, e], op=MULT
+            out=same[:, tokens, :], in0=halves(cos_part[:, tokens, :])[:, e], in1=q_halves[:, e], op=MULT
         )
         nc.vector.tensor_tensor(
-            out=other[:, tokens, :], in0=q_halves[:, 1 - e], in1=halves(sin_part[:, tokens, :])[:, e], op=MULT
+            out=other[:, tokens, :], in0=halves(sin_part[:, tokens, :])[:, e], in1=q_halves[:, 1 - e], op=MULT
         )
     nc.gpsimd.tensor_tensor(
         out=rotated,

@@ -77,12 +77,7 @@ def rope_half(nc, products, q_banks, cos_part, sin_part, e, combine, rotated):
         nc.vector.tensor_tensor(
             out=other[:, tokens, :], in0=halves(sin_part[:, tokens, :])[:, e], in1=q_halves[:, 1 - e], op=MULT
         )
-    nc.gpsimd.tensor_tensor(
-        out=rotated,
-        in0=same[:].rearrange("p j i -> p i j"),
-        in1=other[:].rearrange("p j i -> p i j"),
-        op=combine,
-    )
+    nc.gpsimd.tensor_tensor(out=rotated, in0=same[:], in1=other[:], op=combine)
 
 
 def tile_attention_pb_kernel(tc, Q, V, state, cos, sin, out):
@@ -98,8 +93,10 @@ def tile_attention_pb_kernel(tc, Q, V, state, cos, sin, out):
     with ExitStack() as ctx:
         keep = ctx.enter_context(tc.tile_pool(name="keep", bufs=1))
         loads = ctx.enter_context(tc.tile_pool(name="loads", bufs=3))
+        states = ctx.enter_context(tc.tile_pool(name="states", bufs=4))
         turned_sbuf = ctx.enter_context(tc.tile_pool(name="turned_sbuf", bufs=2 * BANKS))
         products = ctx.enter_context(tc.tile_pool(name="products", bufs=6))
+        rotations = ctx.enter_context(tc.tile_pool(name="rotations", bufs=3))
         quantised = ctx.enter_context(tc.tile_pool(name="quantised", bufs=3))
         results = ctx.enter_context(tc.tile_pool(name="results", bufs=3))
         turned_psum = ctx.enter_context(tc.psum_pool(name="turned_psum", bufs=BANKS))
@@ -122,9 +119,9 @@ def tile_attention_pb_kernel(tc, Q, V, state, cos, sin, out):
         )
 
         q_part, cos_part, sin_part, state_part = {}, {}, {}, {}
-        q_banks, rotated, sums = {}, {}, {}
+        q_banks, rotated, grouped, sums = {}, {}, {}, {}
 
-        for turn in range(-1, PARTS + 2):
+        for turn in range(-1, PARTS + 3):
             u = turn + 1
             if u < PARTS:
                 if u % PARTS_PER_CHUNK == 0:
@@ -137,7 +134,7 @@ def tile_attention_pb_kernel(tc, Q, V, state, cos, sin, out):
                     nc.sync.dma_start(out=cos_sb[:], in_=cos_rows[:, :, features])
                     sin_sb = loads.tile([P, PACK, CHUNK], BF16)
                     nc.sync.dma_start(out=sin_sb[:], in_=sin_rows[:, :, features])
-                    state_sb = loads.tile([P, CHUNK // GROUP, 2 * VALUES], BF16)
+                    state_sb = states.tile([P, CHUNK // GROUP, 2 * VALUES], BF16)
                     nc.sync.dma_start(out=state_sb[:], in_=state_rows[:, groups, :])
                     for h in range(PARTS_PER_CHUNK):
                         q_part[u + h] = q_sb[:, :, h * PART : (h + 1) * PART]
@@ -148,12 +145,19 @@ def tile_attention_pb_kernel(tc, Q, V, state, cos, sin, out):
 
             u = turn
             if 0 <= u < PARTS:
-                rotated_u = quantised.tile([P, 2, HALF, PACK], BF16, align_bytes=64)
+                rotated_u = rotations.tile([P, 2, PACK, HALF], F32)
                 rope_half(nc, products, q_banks[u], cos_part[u], sin_part[u], 0, SUBTRACT, rotated_u[:, 0])
                 rope_half(nc, products, q_banks[u], cos_part[u], sin_part[u], 1, ADD, rotated_u[:, 1])
                 rotated[u] = rotated_u
 
-            u = turn - 2
+            u = turn - 1
+            if 0 <= u < PARTS:
+                grouped_u = quantised.tile([P, 2, HALF, PACK], BF16, align_bytes=64)
+                for e in range(2):
+                    nc.scalar.copy(out=grouped_u[:, e], in_=rotated[u][:, e].rearrange("p j i -> p i j"))
+                grouped[u] = grouped_u
+
+            u = turn - 3
             if 0 <= u < PARTS:
                 new_state = results.tile([P, GROUPS, 2 * VALUES], F32)
                 for g in range(GROUPS):
@@ -167,14 +171,14 @@ def tile_attention_pb_kernel(tc, Q, V, state, cos, sin, out):
                     )
                 nc.scalar.dma_start(out=out_rows[:, u * GROUPS : (u + 1) * GROUPS, :], in_=new_state[:])
 
-            u = turn - 1
+            u = turn - 2
             if 0 <= u < PARTS:
                 codes = quantised.tile([P, 2, HALF], U32, align_bytes=64)
                 scales = quantised.tile([P, 2, HALF], U8, align_bytes=64)
                 nc.vector.quantize_mx(
                     out=codes[:].rearrange("p e i -> p (e i)").bitcast(FP8X4),
                     scales=scales[:].rearrange("p e i -> p (e i)"),
-                    in_=rotated[u][:].rearrange("p e i j -> p (e i j)"),
+                    in_=grouped[u][:].rearrange("p e i j -> p (e i j)"),
                 )
                 sums[u] = []
                 for g in range(GROUPS):

@@ -24,60 +24,18 @@ PART = 512
 PARTS = FEATURES // PART
 PARTS_PER_CHUNK = CHUNK // PART
 HALF = PART // 2
+EVEN, ODD = 0, 1
 GROUP = 2 * P
 GROUPS = PART // GROUP
 BANK_TOKENS = 2
 BANKS = PACK // BANK_TOKENS
-SQUARES = PART // P
+SQUARES = HALF // P
 
 FLOPS = 2 * TOKENS * FEATURES * VALUES
 
 
 def halves(rows):
     return rows.rearrange("p j (i e) -> p e j i", e=2)
-
-
-def q_into_psum(nc, turned_psum, turned_sbuf, q_psum, identity, q_part):
-    turned_back = []
-    copies = []
-    for k in range(BANKS):
-        turned = turned_psum.tile([P, BANK_TOKENS, SQUARES, P], BF16)
-        for j in range(BANK_TOKENS):
-            for s in range(SQUARES):
-                nc.tensor.transpose(
-                    out=turned[:, j, s, :],
-                    in_=q_part[:, k * BANK_TOKENS + j, s * P : (s + 1) * P],
-                    identity=identity,
-                )
-        turned_copy = turned_sbuf.tile([P, BANK_TOKENS, SQUARES, P], BF16)
-        nc.scalar.copy(out=turned_copy[:], in_=turned[:])
-        copies.append(turned_copy)
-    for k in range(BANKS):
-        q_bank = q_psum.tile([P, BANK_TOKENS, PART], BF16)
-        for j in range(BANK_TOKENS):
-            for s in range(SQUARES):
-                nc.tensor.transpose(
-                    out=q_bank[:, j, s * P : (s + 1) * P],
-                    in_=copies[k][:, j, s, :],
-                    identity=identity,
-                )
-        turned_back.append(q_bank)
-    return turned_back
-
-
-def rope_half(nc, products, q_banks, cos_part, sin_part, e, combine, rotated):
-    same = products.tile([P, PACK, HALF], F32)
-    other = products.tile([P, PACK, HALF], F32)
-    for k in range(BANKS):
-        tokens = slice(k * BANK_TOKENS, (k + 1) * BANK_TOKENS)
-        q_halves = halves(q_banks[k][:])
-        nc.vector.tensor_tensor(
-            out=same[:, tokens, :], in0=halves(cos_part[:, tokens, :])[:, e], in1=q_halves[:, e], op=MULT
-        )
-        nc.vector.tensor_tensor(
-            out=other[:, tokens, :], in0=halves(sin_part[:, tokens, :])[:, e], in1=q_halves[:, 1 - e], op=MULT
-        )
-    nc.gpsimd.tensor_tensor(out=rotated, in0=same[:], in1=other[:], op=combine)
 
 
 def tile_attention_pb_kernel(tc, Q, V, state, cos, sin, out):
@@ -103,11 +61,11 @@ def tile_attention_pb_kernel(tc, Q, V, state, cos, sin, out):
         q_psum = ctx.enter_context(tc.psum_pool(name="q_psum", bufs=2 * BANKS))
         sums_psum = ctx.enter_context(tc.psum_pool(name="sums_psum", bufs=GROUPS))
 
-        identity = keep.tile([P, P], BF16)
+        identity = keep.tile([P, P], F32)
         make_identity(nc, identity[:])
 
         v_raw = keep.tile([P, PACK, VALUES], BF16)
-        nc.sync.dma_start(out=v_raw[:], in_=v_rows)
+        nc.scalar.dma_start(out=v_raw[:], in_=v_rows)
         v_grouped = keep.tile([P, VALUES, PACK], BF16, align_bytes=64)
         nc.vector.tensor_copy(out=v_grouped[:], in_=v_raw[:].rearrange("p j d -> p d j"))
         v_codes = keep.tile([P, VALUES], U32, align_bytes=64)
@@ -118,80 +76,126 @@ def tile_attention_pb_kernel(tc, Q, V, state, cos, sin, out):
             in_=v_grouped[:].rearrange("p d j -> p (d j)"),
         )
 
-        q_part, cos_part, sin_part, state_part = {}, {}, {}, {}
+        q_words, cos_part, sin_part, state_part = {}, {}, {}, {}
         q_banks, rotated, grouped, sums = {}, {}, {}, {}
 
-        for turn in range(-1, PARTS + 3):
-            u = turn + 1
-            if u < PARTS:
-                if u % PARTS_PER_CHUNK == 0:
-                    c = u // PARTS_PER_CHUNK
-                    features = slice(c * CHUNK, (c + 1) * CHUNK)
-                    groups = slice(c * CHUNK // GROUP, (c + 1) * CHUNK // GROUP)
-                    q_sb = loads.tile([P, PACK, CHUNK], BF16)
-                    nc.sync.dma_start(out=q_sb[:], in_=q_rows[:, :, features])
-                    cos_sb = loads.tile([P, PACK, CHUNK], BF16)
-                    nc.sync.dma_start(out=cos_sb[:], in_=cos_rows[:, :, features])
-                    sin_sb = loads.tile([P, PACK, CHUNK], BF16)
-                    nc.sync.dma_start(out=sin_sb[:], in_=sin_rows[:, :, features])
-                    state_sb = states.tile([P, CHUNK // GROUP, 2 * VALUES], BF16)
-                    nc.sync.dma_start(out=state_sb[:], in_=state_rows[:, groups, :])
-                    for h in range(PARTS_PER_CHUNK):
-                        q_part[u + h] = q_sb[:, :, h * PART : (h + 1) * PART]
-                        cos_part[u + h] = cos_sb[:, :, h * PART : (h + 1) * PART]
-                        sin_part[u + h] = sin_sb[:, :, h * PART : (h + 1) * PART]
-                        state_part[u + h] = state_sb[:, h * GROUPS : (h + 1) * GROUPS, :]
-                q_banks[u] = q_into_psum(nc, turned_psum, turned_sbuf, q_psum, identity[:], q_part[u])
+        def load_chunk(c):
+            features = slice(c * CHUNK, (c + 1) * CHUNK)
+            groups = slice(c * CHUNK // GROUP, (c + 1) * CHUNK // GROUP)
+            q_sb = loads.tile([P, PACK, CHUNK], BF16)
+            nc.sync.dma_start(out=q_sb[:], in_=q_rows[:, :, features])
+            cos_sb = loads.tile([P, PACK, CHUNK], BF16)
+            nc.sync.dma_start(out=cos_sb[:], in_=cos_rows[:, :, features])
+            sin_sb = loads.tile([P, PACK, CHUNK], BF16)
+            nc.sync.dma_start(out=sin_sb[:], in_=sin_rows[:, :, features])
+            state_sb = states.tile([P, CHUNK // GROUP, 2 * VALUES], BF16)
+            nc.sync.dma_start(out=state_sb[:], in_=state_rows[:, groups, :])
+            for h in range(PARTS_PER_CHUNK):
+                u = c * PARTS_PER_CHUNK + h
+                q_words[u] = q_sb[:].bitcast(F32)[:, :, h * HALF : (h + 1) * HALF]
+                cos_part[u] = cos_sb[:, :, h * PART : (h + 1) * PART]
+                sin_part[u] = sin_sb[:, :, h * PART : (h + 1) * PART]
+                state_part[u] = state_sb[:, h * GROUPS : (h + 1) * GROUPS, :]
 
-            u = turn
-            if 0 <= u < PARTS:
-                rotated_u = rotations.tile([P, 2, PACK, HALF], F32)
-                rope_half(nc, products, q_banks[u], cos_part[u], sin_part[u], 0, SUBTRACT, rotated_u[:, 0])
-                rope_half(nc, products, q_banks[u], cos_part[u], sin_part[u], 1, ADD, rotated_u[:, 1])
-                rotated[u] = rotated_u
-
-            u = turn - 1
-            if 0 <= u < PARTS:
-                grouped_u = quantised.tile([P, 2, HALF, PACK], BF16, align_bytes=64)
-                for e in range(2):
-                    nc.scalar.copy(out=grouped_u[:, e], in_=rotated[u][:, e].rearrange("p j i -> p i j"))
-                grouped[u] = grouped_u
-
-            u = turn - 3
-            if 0 <= u < PARTS:
-                new_state = results.tile([P, GROUPS, 2 * VALUES], F32)
-                for g in range(GROUPS):
-                    nc.vector.scalar_tensor_tensor(
-                        out=new_state[:, g, :],
-                        in0=sums[u][g][:].rearrange("m e d -> m (e d)"),
-                        scalar=SCALE,
-                        in1=state_part[u][:, g, :],
-                        op0=MULT,
-                        op1=ADD,
-                    )
-                nc.scalar.dma_start(out=out_rows[:, u * GROUPS : (u + 1) * GROUPS, :], in_=new_state[:])
-
-            u = turn - 2
-            if 0 <= u < PARTS:
-                codes = quantised.tile([P, 2, HALF], U32, align_bytes=64)
-                scales = quantised.tile([P, 2, HALF], U8, align_bytes=64)
-                nc.vector.quantize_mx(
-                    out=codes[:].rearrange("p e i -> p (e i)").bitcast(FP8X4),
-                    scales=scales[:].rearrange("p e i -> p (e i)"),
-                    in_=grouped[u][:].rearrange("p e i j -> p (e i j)"),
-                )
-                sums[u] = []
-                for g in range(GROUPS):
-                    pairs = slice(g * P, (g + 1) * P)
-                    acc = sums_psum.tile([P, 2, VALUES], F32)
-                    for e in range(2):
-                        nc.tensor.matmul_mx(
-                            out=acc[:, e, :],
-                            lhsT=codes[:, e, pairs].bitcast(FP8X4),
-                            lhsT_scale=scales[:, e, pairs],
-                            rhs=v_codes[:].bitcast(FP8X4),
-                            rhs_scale=v_scales[:],
-                            start=True,
-                            stop=True,
+        def q_into_psum(u):
+            copies = []
+            for k in range(BANKS):
+                turned = turned_psum.tile([P, BANK_TOKENS, SQUARES, P], F32)
+                for j in range(BANK_TOKENS):
+                    for s in range(SQUARES):
+                        nc.tensor.transpose(
+                            out=turned[:, j, s, :],
+                            in_=q_words[u][:, k * BANK_TOKENS + j, s * P : (s + 1) * P],
+                            identity=identity[:],
                         )
-                    sums[u].append(acc)
+                turned_copy = turned_sbuf.tile([P, BANK_TOKENS, SQUARES, 2 * P], BF16)
+                nc.scalar.copy(out=turned_copy[:], in_=turned[:].bitcast(BF16))
+                copies.append(turned_copy)
+            q_banks[u] = []
+            for k in range(BANKS):
+                q_bank = q_psum.tile([P, BANK_TOKENS, HALF], F32)
+                for j in range(BANK_TOKENS):
+                    for s in range(SQUARES):
+                        nc.tensor.transpose(
+                            out=q_bank[:, j, s * P : (s + 1) * P],
+                            in_=copies[k][:].bitcast(F32)[:, j, s, :],
+                            identity=identity[:],
+                        )
+                q_banks[u].append(q_bank)
+
+        def rope_half(u, e, combine):
+            same = products.tile([P, PACK, HALF], F32)
+            other = products.tile([P, PACK, HALF], F32)
+            for k in range(BANKS):
+                tokens = slice(k * BANK_TOKENS, (k + 1) * BANK_TOKENS)
+                q_halves = halves(q_banks[u][k][:].bitcast(BF16))
+                nc.vector.tensor_tensor(
+                    out=same[:, tokens, :], in0=halves(cos_part[u][:, tokens, :])[:, e], in1=q_halves[:, e], op=MULT
+                )
+                nc.vector.tensor_tensor(
+                    out=other[:, tokens, :],
+                    in0=halves(sin_part[u][:, tokens, :])[:, e],
+                    in1=q_halves[:, 1 - e],
+                    op=MULT,
+                )
+            nc.gpsimd.tensor_tensor(out=rotated[u][:, e], in0=same[:], in1=other[:], op=combine)
+
+        def round_and_regroup(u):
+            grouped[u] = quantised.tile([P, 2, HALF, PACK], BF16, align_bytes=64, name="grouped")
+            for e in (EVEN, ODD):
+                nc.scalar.copy(out=grouped[u][:, e], in_=rotated[u][:, e].rearrange("p j i -> p i j"))
+
+        def quantise_and_multiply(u):
+            codes = quantised.tile([P, 2, HALF], U32, align_bytes=64)
+            scales = quantised.tile([P, 2, HALF], U8, align_bytes=64)
+            nc.vector.quantize_mx(
+                out=codes[:].rearrange("p e i -> p (e i)").bitcast(FP8X4),
+                scales=scales[:].rearrange("p e i -> p (e i)"),
+                in_=grouped[u][:].rearrange("p e i j -> p (e i j)"),
+            )
+            sums[u] = []
+            for g in range(GROUPS):
+                pairs = slice(g * P, (g + 1) * P)
+                acc = sums_psum.tile([P, 2, VALUES], F32)
+                for e in (EVEN, ODD):
+                    nc.tensor.matmul_mx(
+                        out=acc[:, e, :],
+                        lhsT=codes[:, e, pairs].bitcast(FP8X4),
+                        lhsT_scale=scales[:, e, pairs],
+                        rhs=v_codes[:].bitcast(FP8X4),
+                        rhs_scale=v_scales[:],
+                        start=True,
+                        stop=True,
+                    )
+                sums[u].append(acc)
+
+        def add_to_state(u):
+            new_state = results.tile([P, GROUPS, 2 * VALUES], F32)
+            for g in range(GROUPS):
+                nc.vector.scalar_tensor_tensor(
+                    out=new_state[:, g, :],
+                    in0=sums[u][g][:].rearrange("m e d -> m (e d)"),
+                    scalar=SCALE,
+                    in1=state_part[u][:, g, :],
+                    op0=MULT,
+                    op1=ADD,
+                )
+            nc.scalar.dma_start(out=out_rows[:, u * GROUPS : (u + 1) * GROUPS, :], in_=new_state[:])
+
+        with tc.manual_schedule():
+            for turn in range(-1, PARTS + 3):
+                if turn + 1 < PARTS:
+                    if (turn + 1) % PARTS_PER_CHUNK == 0:
+                        load_chunk((turn + 1) // PARTS_PER_CHUNK)
+                    q_into_psum(turn + 1)
+                if 0 <= turn < PARTS:
+                    rotated[turn] = rotations.tile([P, 2, PACK, HALF], F32, name="rotated")
+                    rope_half(turn, EVEN, SUBTRACT)
+                if 0 <= turn - 2 < PARTS:
+                    quantise_and_multiply(turn - 2)
+                if 0 <= turn < PARTS:
+                    rope_half(turn, ODD, ADD)
+                if 0 <= turn - 1 < PARTS:
+                    round_and_regroup(turn - 1)
+                if 0 <= turn - 3 < PARTS:
+                    add_to_state(turn - 3)

@@ -79,19 +79,19 @@ def tile_attention_pb_kernel(tc, Q, V, state, cos, sin, out):
         q_words, cos_part, sin_part, state_part = {}, {}, {}, {}
         q_banks, rotated, grouped, sums = {}, {}, {}, {}
 
-        def load_chunk(c):
-            features = slice(c * CHUNK, (c + 1) * CHUNK)
-            groups = slice(c * CHUNK // GROUP, (c + 1) * CHUNK // GROUP)
-            q_sb = loads.tile([P, PACK, CHUNK], BF16)
+        def load(first, parts):
+            features = slice(first * PART, (first + parts) * PART)
+            groups = slice(first * GROUPS, (first + parts) * GROUPS)
+            q_sb = loads.tile([P, PACK, parts * PART], BF16)
             nc.sync.dma_start(out=q_sb[:], in_=q_rows[:, :, features])
-            cos_sb = loads.tile([P, PACK, CHUNK], BF16)
+            cos_sb = loads.tile([P, PACK, parts * PART], BF16)
             nc.sync.dma_start(out=cos_sb[:], in_=cos_rows[:, :, features])
-            sin_sb = loads.tile([P, PACK, CHUNK], BF16)
+            sin_sb = loads.tile([P, PACK, parts * PART], BF16)
             nc.sync.dma_start(out=sin_sb[:], in_=sin_rows[:, :, features])
-            state_sb = states.tile([P, CHUNK // GROUP, 2 * VALUES], BF16)
+            state_sb = states.tile([P, parts * GROUPS, 2 * VALUES], BF16)
             nc.sync.dma_start(out=state_sb[:], in_=state_rows[:, groups, :])
-            for h in range(PARTS_PER_CHUNK):
-                u = c * PARTS_PER_CHUNK + h
+            for h in range(parts):
+                u = first + h
                 q_words[u] = q_sb[:].bitcast(F32)[:, :, h * HALF : (h + 1) * HALF]
                 cos_part[u] = cos_sb[:, :, h * PART : (h + 1) * PART]
                 sin_part[u] = sin_sb[:, :, h * PART : (h + 1) * PART]
@@ -180,14 +180,18 @@ def tile_attention_pb_kernel(tc, Q, V, state, cos, sin, out):
                     op0=MULT,
                     op1=ADD,
                 )
-            nc.scalar.dma_start(out=out_rows[:, u * GROUPS : (u + 1) * GROUPS, :], in_=new_state[:])
+                nc.scalar.dma_start(out=out_rows[:, u * GROUPS + g, :], in_=new_state[:, g, :])
 
         with tc.manual_schedule():
             for turn in range(-1, PARTS + 3):
                 if turn + 1 < PARTS:
-                    if (turn + 1) % PARTS_PER_CHUNK == 0:
-                        load_chunk((turn + 1) // PARTS_PER_CHUNK)
+                    if turn + 1 < PARTS_PER_CHUNK:
+                        load(turn + 1, 1)
+                    elif (turn + 1) % PARTS_PER_CHUNK == 0:
+                        load(turn + 1, PARTS_PER_CHUNK)
                     q_into_psum(turn + 1)
+                if 0 <= turn - 3 < PARTS:
+                    add_to_state(turn - 3)
                 if 0 <= turn < PARTS:
                     rotated[turn] = rotations.tile([P, 2, PACK, HALF], F32, name="rotated")
                     rope_half(turn, EVEN, SUBTRACT)
@@ -197,5 +201,3 @@ def tile_attention_pb_kernel(tc, Q, V, state, cos, sin, out):
                     rope_half(turn, ODD, ADD)
                 if 0 <= turn - 1 < PARTS:
                     round_and_regroup(turn - 1)
-                if 0 <= turn - 3 < PARTS:
-                    add_to_state(turn - 3)

@@ -53,7 +53,7 @@ def tile_attention_pb_kernel(tc, Q, V, state, cos, sin, out):
         loads = ctx.enter_context(tc.tile_pool(name="loads", bufs=3))
         states = ctx.enter_context(tc.tile_pool(name="states", bufs=4))
         turned_sbuf = ctx.enter_context(tc.tile_pool(name="turned_sbuf", bufs=2 * BANKS))
-        products = ctx.enter_context(tc.tile_pool(name="products", bufs=6))
+        products = ctx.enter_context(tc.tile_pool(name="products", bufs=3))
         rotations = ctx.enter_context(tc.tile_pool(name="rotations", bufs=3))
         quantised = ctx.enter_context(tc.tile_pool(name="quantised", bufs=3))
         results = ctx.enter_context(tc.tile_pool(name="results", bufs=3))
@@ -77,7 +77,7 @@ def tile_attention_pb_kernel(tc, Q, V, state, cos, sin, out):
         )
 
         q_words, cos_part, sin_part, state_part = {}, {}, {}, {}
-        q_banks, rotated, grouped, sums = {}, {}, {}, {}
+        q_banks, same, other, rotated, grouped, sums = {}, {}, {}, {}, {}, {}
 
         def load(first, parts):
             features = slice(first * PART, (first + parts) * PART)
@@ -123,22 +123,23 @@ def tile_attention_pb_kernel(tc, Q, V, state, cos, sin, out):
                         )
                 q_banks[u].append(q_bank)
 
-        def rope_half(u, e, combine):
-            same = products.tile([P, PACK, HALF], F32)
-            other = products.tile([P, PACK, HALF], F32)
-            for k in range(BANKS):
-                tokens = slice(k * BANK_TOKENS, (k + 1) * BANK_TOKENS)
-                q_halves = halves(q_banks[u][k][:].bitcast(BF16))
-                nc.vector.tensor_tensor(
-                    out=same[:, tokens, :], in0=halves(cos_part[u][:, tokens, :])[:, e], in1=q_halves[:, e], op=MULT
-                )
-                nc.vector.tensor_tensor(
-                    out=other[:, tokens, :],
-                    in0=halves(sin_part[u][:, tokens, :])[:, e],
-                    in1=q_halves[:, 1 - e],
-                    op=MULT,
-                )
-            nc.gpsimd.tensor_tensor(out=rotated[u][:, e], in0=same[:], in1=other[:], op=combine)
+        def rope_products(u, k):
+            if k == 0:
+                same[u] = products.tile([P, 2, PACK, HALF], F32, name="same")
+                other[u] = products.tile([P, 2, PACK, HALF], F32, name="other")
+            tokens = slice(k * BANK_TOKENS, (k + 1) * BANK_TOKENS)
+            q_halves = halves(q_banks[u][k][:].bitcast(BF16))
+            nc.vector.tensor_tensor(
+                out=same[u][:, :, tokens, :], in0=halves(cos_part[u][:, tokens, :]), in1=q_halves, op=MULT
+            )
+            nc.vector.tensor_tensor(
+                out=other[u][:, :, tokens, :], in0=halves(sin_part[u][:, tokens, :]), in1=q_halves[:, ::-1], op=MULT
+            )
+
+        def rope_sums(u):
+            rotated[u] = rotations.tile([P, 2, PACK, HALF], F32, name="rotated")
+            for e, combine in ((EVEN, SUBTRACT), (ODD, ADD)):
+                nc.gpsimd.tensor_tensor(out=rotated[u][:, e], in0=same[u][:, e], in1=other[u][:, e], op=combine)
 
         def round_and_regroup(u):
             grouped[u] = quantised.tile([P, 2, HALF, PACK], BF16, align_bytes=64, name="grouped")
@@ -190,14 +191,15 @@ def tile_attention_pb_kernel(tc, Q, V, state, cos, sin, out):
                     elif (turn + 1) % PARTS_PER_CHUNK == 0:
                         load(turn + 1, PARTS_PER_CHUNK)
                     q_into_psum(turn + 1)
+                if 0 <= turn < PARTS:
+                    rope_products(turn, 0)
                 if 0 <= turn - 3 < PARTS:
                     add_to_state(turn - 3)
                 if 0 <= turn < PARTS:
-                    rotated[turn] = rotations.tile([P, 2, PACK, HALF], F32, name="rotated")
-                    rope_half(turn, EVEN, SUBTRACT)
+                    rope_products(turn, 1)
                 if 0 <= turn - 2 < PARTS:
                     quantise_and_multiply(turn - 2)
                 if 0 <= turn < PARTS:
-                    rope_half(turn, ODD, ADD)
+                    rope_sums(turn)
                 if 0 <= turn - 1 < PARTS:
                     round_and_regroup(turn - 1)

@@ -10,7 +10,6 @@ U8 = mybir.dt.uint8
 FP8X4 = mybir.dt.float8_e4m3fn_x4
 MULT = mybir.AluOpType.mult
 ADD = mybir.AluOpType.add
-SUBTRACT = mybir.AluOpType.subtract
 
 P = 128
 PACK = 4
@@ -19,23 +18,16 @@ FEATURES = 8192
 VALUES = 256
 SCALE = FEATURES**-0.5
 
-CHUNK = 1024
-PART = 512
-PARTS = FEATURES // PART
-PARTS_PER_CHUNK = CHUNK // PART
-HALF = PART // 2
+UNIT = 2 * P
+UNITS = FEATURES // UNIT
 EVEN, ODD = 0, 1
-GROUP = 2 * P
-GROUPS = PART // GROUP
-BANK_TOKENS = 2
-BANKS = PACK // BANK_TOKENS
-SQUARES = HALF // P
+LOAD_UNITS = (1, 1, 2) + (4,) * 7
+assert sum(LOAD_UNITS) == UNITS
+LOAD_BUFS = 4
+STATE_BUFS = 5
+LOAD_AHEAD = 8
 
 FLOPS = 2 * TOKENS * FEATURES * VALUES
-
-
-def halves(rows):
-    return rows.rearrange("p j (i e) -> p e j i", e=2)
 
 
 def tile_attention_pb_kernel(tc, Q, V, state, cos, sin, out):
@@ -45,21 +37,21 @@ def tile_attention_pb_kernel(tc, Q, V, state, cos, sin, out):
     cos_rows = cos.rearrange("(p j) f -> p j f", j=PACK)
     sin_rows = sin.rearrange("(p j) f -> p j f", j=PACK)
     v_rows = V.flatten_outer_dims().rearrange("(p j) d -> p j d", j=PACK)
-    state_rows = state.flatten_outer_dims().rearrange("(n m e) d -> m n (e d)", m=P, e=2)
-    out_rows = out.flatten_outer_dims().rearrange("(n m e) d -> m n (e d)", m=P, e=2)
+    state_rows = state.flatten_outer_dims().rearrange("(n i e) d -> i n (e d)", i=P, e=2)
+    out_rows = out.flatten_outer_dims().rearrange("(n i e) d -> i n (e d)", i=P, e=2)
 
     with ExitStack() as ctx:
         keep = ctx.enter_context(tc.tile_pool(name="keep", bufs=1))
-        loads = ctx.enter_context(tc.tile_pool(name="loads", bufs=3))
-        states = ctx.enter_context(tc.tile_pool(name="states", bufs=4))
-        turned_sbuf = ctx.enter_context(tc.tile_pool(name="turned_sbuf", bufs=2 * BANKS))
+        loads = ctx.enter_context(tc.tile_pool(name="loads", bufs=LOAD_BUFS))
+        states = ctx.enter_context(tc.tile_pool(name="states", bufs=STATE_BUFS))
+        turned_q = ctx.enter_context(tc.tile_pool(name="turned_q", bufs=4))
         products = ctx.enter_context(tc.tile_pool(name="products", bufs=3))
-        rotations = ctx.enter_context(tc.tile_pool(name="rotations", bufs=3))
         quantised = ctx.enter_context(tc.tile_pool(name="quantised", bufs=3))
-        results = ctx.enter_context(tc.tile_pool(name="results", bufs=3))
-        turned_psum = ctx.enter_context(tc.psum_pool(name="turned_psum", bufs=BANKS))
-        q_psum = ctx.enter_context(tc.psum_pool(name="q_psum", bufs=2 * BANKS))
-        sums_psum = ctx.enter_context(tc.psum_pool(name="sums_psum", bufs=GROUPS))
+        results = ctx.enter_context(tc.tile_pool(name="results", bufs=4))
+        q_psum = ctx.enter_context(tc.psum_pool(name="q_psum", bufs=1))
+        table_psum = ctx.enter_context(tc.psum_pool(name="table_psum", bufs=3))
+        rope_psum = ctx.enter_context(tc.psum_pool(name="rope_psum", bufs=2))
+        sums_psum = ctx.enter_context(tc.psum_pool(name="sums_psum", bufs=2))
 
         identity = keep.tile([P, P], F32)
         make_identity(nc, identity[:])
@@ -76,130 +68,145 @@ def tile_attention_pb_kernel(tc, Q, V, state, cos, sin, out):
             in_=v_grouped[:].rearrange("p d j -> p (d j)"),
         )
 
-        q_words, cos_part, sin_part, state_part = {}, {}, {}, {}
-        q_banks, same, other, rotated, grouped, sums = {}, {}, {}, {}, {}, {}
+        q_words, cos_words, sin_words, state_unit = {}, {}, {}, {}
+        q_turned, cos_turned, sin_turned = {}, {}, {}
+        same, other, grouped, codes, scales, sums, new_state = {}, {}, {}, {}, {}, {}, {}
 
-        def load(first, parts):
-            features = slice(first * PART, (first + parts) * PART)
-            groups = slice(first * GROUPS, (first + parts) * GROUPS)
-            q_sb = loads.tile([P, PACK, parts * PART], BF16)
+        def load(first, units):
+            features = slice(first * UNIT, (first + units) * UNIT)
+            q_sb = loads.tile([P, PACK, units * UNIT], BF16)
             nc.sync.dma_start(out=q_sb[:], in_=q_rows[:, :, features])
-            cos_sb = loads.tile([P, PACK, parts * PART], BF16)
+            cos_sb = loads.tile([P, PACK, units * UNIT], BF16)
             nc.sync.dma_start(out=cos_sb[:], in_=cos_rows[:, :, features])
-            sin_sb = loads.tile([P, PACK, parts * PART], BF16)
+            sin_sb = loads.tile([P, PACK, units * UNIT], BF16)
             nc.sync.dma_start(out=sin_sb[:], in_=sin_rows[:, :, features])
-            state_sb = states.tile([P, parts * GROUPS, 2 * VALUES], BF16)
-            nc.sync.dma_start(out=state_sb[:], in_=state_rows[:, groups, :])
-            for h in range(parts):
-                u = first + h
-                q_words[u] = q_sb[:].bitcast(F32)[:, :, h * HALF : (h + 1) * HALF]
-                cos_part[u] = cos_sb[:, :, h * PART : (h + 1) * PART]
-                sin_part[u] = sin_sb[:, :, h * PART : (h + 1) * PART]
-                state_part[u] = state_sb[:, h * GROUPS : (h + 1) * GROUPS, :]
+            state_sb = states.tile([P, units, 2 * VALUES], BF16)
+            nc.sync.dma_start(out=state_sb[:], in_=state_rows[:, first : first + units, :])
+            for h in range(units):
+                words = slice(h * P, (h + 1) * P)
+                q_words[first + h] = q_sb[:].bitcast(F32)[:, :, words]
+                cos_words[first + h] = cos_sb[:].bitcast(F32)[:, :, words]
+                sin_words[first + h] = sin_sb[:].bitcast(F32)[:, :, words]
+                state_unit[first + h] = state_sb[:, h, :]
 
-        def q_into_psum(u):
-            copies = []
-            for k in range(BANKS):
-                turned = turned_psum.tile([P, BANK_TOKENS, SQUARES, P], F32)
-                for j in range(BANK_TOKENS):
-                    for s in range(SQUARES):
-                        nc.tensor.transpose(
-                            out=turned[:, j, s, :],
-                            in_=q_words[u][:, k * BANK_TOKENS + j, s * P : (s + 1) * P],
-                            identity=identity[:],
-                        )
-                turned_copy = turned_sbuf.tile([P, BANK_TOKENS, SQUARES, 2 * P], BF16)
-                nc.scalar.copy(out=turned_copy[:], in_=turned[:].bitcast(BF16))
-                copies.append(turned_copy)
-            q_banks[u] = []
-            for k in range(BANKS):
-                q_bank = q_psum.tile([P, BANK_TOKENS, HALF], F32)
-                for j in range(BANK_TOKENS):
-                    for s in range(SQUARES):
-                        nc.tensor.transpose(
-                            out=q_bank[:, j, s * P : (s + 1) * P],
-                            in_=copies[k][:].bitcast(F32)[:, j, s, :],
-                            identity=identity[:],
-                        )
-                q_banks[u].append(q_bank)
+        def turn_words(bank, words):
+            for j in range(PACK):
+                nc.tensor.transpose(out=bank[:, j, :], in_=words[:, j, :], identity=identity[:])
 
-        def rope_products(u, k):
-            if k == 0:
-                same[u] = products.tile([P, 2, PACK, HALF], F32, name="same")
-                other[u] = products.tile([P, 2, PACK, HALF], F32, name="other")
-            tokens = slice(k * BANK_TOKENS, (k + 1) * BANK_TOKENS)
-            q_halves = halves(q_banks[u][k][:].bitcast(BF16))
-            nc.vector.tensor_tensor(
-                out=same[u][:, :, tokens, :], in0=halves(cos_part[u][:, tokens, :]), in1=q_halves, op=MULT
+        def by_half(turned):
+            return turned.rearrange("i j (p e) -> i j e p", e=2)
+
+        def turn_q(u):
+            bank = q_psum.tile([P, PACK, P], F32, name="q_bank")
+            turn_words(bank, q_words[u])
+            q_turned[u] = turned_q.tile([P, PACK, 2 * P], BF16, name="q_turned")
+            nc.scalar.copy(out=q_turned[u][:], in_=bank[:].bitcast(BF16))
+
+        def turn_table(turned, words, u):
+            turned[u] = table_psum.tile([P, PACK, P], F32, name="table_bank")
+            turn_words(turned[u], words[u])
+
+        def multiply_rope(u):
+            q_halves = by_half(q_turned[u][:])
+            cos_halves = by_half(cos_turned[u][:].bitcast(BF16))
+            sin_halves = by_half(sin_turned[u][:].bitcast(BF16))
+            same[u] = products.tile([P, PACK, 2, P], F32, name="same")
+            other[u] = products.tile([P, PACK, 2, P], F32, name="other")
+            nc.vector.tensor_tensor(out=same[u][:], in0=cos_halves, in1=q_halves, op=MULT)
+            nc.vector.scalar_tensor_tensor(
+                out=other[u][:, :, EVEN, :],
+                in0=sin_halves[:, :, EVEN, :],
+                scalar=-1.0,
+                in1=q_halves[:, :, ODD, :],
+                op0=MULT,
+                op1=MULT,
             )
             nc.vector.tensor_tensor(
-                out=other[u][:, :, tokens, :], in0=halves(sin_part[u][:, tokens, :]), in1=q_halves[:, ::-1], op=MULT
+                out=other[u][:, :, ODD, :], in0=sin_halves[:, :, ODD, :], in1=q_halves[:, :, EVEN, :], op=MULT
             )
 
-        def rope_sums(u):
-            rotated[u] = rotations.tile([P, 2, PACK, HALF], F32, name="rotated")
-            for e, combine in ((EVEN, SUBTRACT), (ODD, ADD)):
-                nc.gpsimd.tensor_tensor(out=rotated[u][:, e], in0=same[u][:, e], in1=other[u][:, e], op=combine)
-
-        def round_and_regroup(u):
-            grouped[u] = quantised.tile([P, 2, HALF, PACK], BF16, align_bytes=64, name="grouped")
+        def add_rope(u):
+            grouped[u] = quantised.tile([P, 2, P, PACK], BF16, align_bytes=64, name="grouped")
             for e in (EVEN, ODD):
-                nc.scalar.copy(out=grouped[u][:, e], in_=rotated[u][:, e].rearrange("p j i -> p i j"))
+                bank = rope_psum.tile([P, PACK, P], F32, name="rope_bank")
+                for j in range(PACK):
+                    nc.tensor.matmul(
+                        out=bank[:, j, :], lhsT=same[u][:, j, e, :], rhs=identity[:], is_transpose=True, start=True, stop=False
+                    )
+                    nc.tensor.matmul(
+                        out=bank[:, j, :], lhsT=other[u][:, j, e, :], rhs=identity[:], is_transpose=True, start=False, stop=True
+                    )
+                nc.scalar.copy(out=grouped[u][:, e], in_=bank[:].rearrange("p j i -> p i j"))
 
-        def quantise_and_multiply(u):
-            codes = quantised.tile([P, 2, HALF], U32, align_bytes=64)
-            scales = quantised.tile([P, 2, HALF], U8, align_bytes=64)
+        def quantise(u):
+            codes[u] = quantised.tile([P, 2, P], U32, align_bytes=64, name="codes")
+            scales[u] = quantised.tile([P, 2, P], U8, align_bytes=64, name="scales")
             nc.vector.quantize_mx(
-                out=codes[:].rearrange("p e i -> p (e i)").bitcast(FP8X4),
-                scales=scales[:].rearrange("p e i -> p (e i)"),
+                out=codes[u][:].rearrange("p e i -> p (e i)").bitcast(FP8X4),
+                scales=scales[u][:].rearrange("p e i -> p (e i)"),
                 in_=grouped[u][:].rearrange("p e i j -> p (e i j)"),
             )
-            sums[u] = []
-            for g in range(GROUPS):
-                pairs = slice(g * P, (g + 1) * P)
-                acc = sums_psum.tile([P, 2, VALUES], F32)
-                for e in (EVEN, ODD):
-                    nc.tensor.matmul_mx(
-                        out=acc[:, e, :],
-                        lhsT=codes[:, e, pairs].bitcast(FP8X4),
-                        lhsT_scale=scales[:, e, pairs],
-                        rhs=v_codes[:].bitcast(FP8X4),
-                        rhs_scale=v_scales[:],
-                        start=True,
-                        stop=True,
-                    )
-                sums[u].append(acc)
+
+        def multiply(u):
+            sums[u] = sums_psum.tile([P, 2, VALUES], F32, name="sums")
+            for e in (EVEN, ODD):
+                nc.tensor.matmul_mx(
+                    out=sums[u][:, e, :],
+                    lhsT=codes[u][:, e, :].bitcast(FP8X4),
+                    lhsT_scale=scales[u][:, e, :],
+                    rhs=v_codes[:].bitcast(FP8X4),
+                    rhs_scale=v_scales[:],
+                    start=True,
+                    stop=True,
+                )
 
         def add_to_state(u):
-            new_state = results.tile([P, GROUPS, 2 * VALUES], F32)
-            for g in range(GROUPS):
-                nc.vector.scalar_tensor_tensor(
-                    out=new_state[:, g, :],
-                    in0=sums[u][g][:].rearrange("m e d -> m (e d)"),
-                    scalar=SCALE,
-                    in1=state_part[u][:, g, :],
-                    op0=MULT,
-                    op1=ADD,
-                )
-                nc.scalar.dma_start(out=out_rows[:, u * GROUPS + g, :], in_=new_state[:, g, :])
+            new_state[u] = results.tile([P, 2 * VALUES], F32, name="new_state")
+            nc.vector.scalar_tensor_tensor(
+                out=new_state[u][:],
+                in0=sums[u][:].rearrange("i e d -> i (e d)"),
+                scalar=SCALE,
+                in1=state_unit[u],
+                op0=MULT,
+                op1=ADD,
+            )
+
+        def store(u):
+            nc.scalar.dma_start(out=out_rows[:, u, :], in_=new_state[u][:])
+
+        first_turn = -2
+        load_turn = {}
+        firsts = [sum(LOAD_UNITS[:n]) for n in range(len(LOAD_UNITS))]
+        for n, first in enumerate(firsts):
+            at = max(first_turn, first - 2 - LOAD_AHEAD)
+            if n >= LOAD_BUFS:
+                at = max(at, firsts[n - LOAD_BUFS] + LOAD_UNITS[n - LOAD_BUFS] - 1)
+            if n >= STATE_BUFS:
+                at = max(at, firsts[n - STATE_BUFS] + LOAD_UNITS[n - STATE_BUFS] + 3)
+            load_turn.setdefault(at, []).append(n)
+
+        def within(u):
+            return 0 <= u < UNITS
 
         with tc.manual_schedule():
-            for turn in range(-1, PARTS + 3):
-                if turn + 1 < PARTS:
-                    if turn + 1 < PARTS_PER_CHUNK:
-                        load(turn + 1, 1)
-                    elif (turn + 1) % PARTS_PER_CHUNK == 0:
-                        load(turn + 1, PARTS_PER_CHUNK)
-                    q_into_psum(turn + 1)
-                if 0 <= turn < PARTS:
-                    rope_products(turn, 0)
-                if 0 <= turn - 3 < PARTS:
+            for turn in range(first_turn, UNITS + 5):
+                for n in load_turn.get(turn, []):
+                    load(firsts[n], LOAD_UNITS[n])
+                if within(turn - 4):
+                    store(turn - 4)
+                if within(turn - 3):
+                    multiply(turn - 3)
+                if within(turn - 1):
+                    add_rope(turn - 1)
+                if within(turn + 1):
+                    turn_table(cos_turned, cos_words, turn + 1)
+                if within(turn + 2):
+                    turn_q(turn + 2)
+                if within(turn + 1):
+                    turn_table(sin_turned, sin_words, turn + 1)
+                if within(turn):
+                    multiply_rope(turn)
+                if within(turn - 2):
+                    quantise(turn - 2)
+                if within(turn - 3):
                     add_to_state(turn - 3)
-                if 0 <= turn < PARTS:
-                    rope_products(turn, 1)
-                if 0 <= turn - 2 < PARTS:
-                    quantise_and_multiply(turn - 2)
-                if 0 <= turn < PARTS:
-                    rope_sums(turn)
-                if 0 <= turn - 1 < PARTS:
-                    round_and_regroup(turn - 1)

@@ -10,6 +10,7 @@ U8 = mybir.dt.uint8
 FP8X4 = mybir.dt.float8_e4m3fn_x4
 MULT = mybir.AluOpType.mult
 ADD = mybir.AluOpType.add
+SUBTRACT = mybir.AluOpType.subtract
 
 P = 128
 PACK = 4
@@ -20,14 +21,47 @@ SCALE = FEATURES**-0.5
 
 UNIT = 2 * P
 UNITS = FEATURES // UNIT
+CHUNK = 4
+CHUNKS = UNITS // CHUNK
+TURNED = CHUNK - 1
+TURNS = CHUNKS * TURNED
 EVEN, ODD = 0, 1
-LOAD_UNITS = (1, 1, 2) + (4,) * 7
+GROUPED_BYTES = CHUNK * UNIT * PACK * 2
+LOAD_UNITS = (1, 1, 2) + (CHUNK,) * (CHUNKS - 1)
 assert sum(LOAD_UNITS) == UNITS
 LOAD_BUFS = 4
 STATE_BUFS = 5
-LOAD_AHEAD = 8
+LOAD_AHEAD = 6
+FIRST_TURN = -2
 
 FLOPS = 2 * TOKENS * FEATURES * VALUES
+
+
+def unit_of_turn(v):
+    return CHUNK * (v // TURNED) + v % TURNED
+
+
+def first_use(u):
+    k, s = divmod(u, CHUNK)
+    return TURNED * k - 2 if s == TURNED else TURNED * k + s - 2
+
+
+def last_use(u):
+    k, s = divmod(u, CHUNK)
+    return TURNED * k - 2 if s == TURNED else TURNED * k + s - 1
+
+
+def state_use(u):
+    k, s = divmod(u, CHUNK)
+    return TURNED * k + 5 + s // 2
+
+
+def halves(rows):
+    return rows.rearrange("p j (i e) -> p e j i", e=2)
+
+
+def by_half(turned):
+    return turned.rearrange("i j (p e) -> i j e p", e=2)
 
 
 def tile_attention_pb_kernel(tc, Q, V, state, cos, sin, out):
@@ -46,8 +80,10 @@ def tile_attention_pb_kernel(tc, Q, V, state, cos, sin, out):
         states = ctx.enter_context(tc.tile_pool(name="states", bufs=STATE_BUFS))
         turned_q = ctx.enter_context(tc.tile_pool(name="turned_q", bufs=4))
         products = ctx.enter_context(tc.tile_pool(name="products", bufs=3))
-        quantised = ctx.enter_context(tc.tile_pool(name="quantised", bufs=3))
-        results = ctx.enter_context(tc.tile_pool(name="results", bufs=4))
+        turnstile = ctx.enter_context(tc.tile_pool(name="turnstile", bufs=1))
+        gpsimd_work = ctx.enter_context(tc.tile_pool(name="gpsimd_work", bufs=2))
+        quantised = ctx.enter_context(tc.tile_pool(name="quantised", bufs=2))
+        results = ctx.enter_context(tc.tile_pool(name="results", bufs=3))
         q_psum = ctx.enter_context(tc.psum_pool(name="q_psum", bufs=1))
         table_psum = ctx.enter_context(tc.psum_pool(name="table_psum", bufs=3))
         rope_psum = ctx.enter_context(tc.psum_pool(name="rope_psum", bufs=2))
@@ -68,9 +104,9 @@ def tile_attention_pb_kernel(tc, Q, V, state, cos, sin, out):
             in_=v_grouped[:].rearrange("p d j -> p (d j)"),
         )
 
-        q_words, cos_words, sin_words, state_unit = {}, {}, {}, {}
-        q_turned, cos_turned, sin_turned = {}, {}, {}
-        same, other, grouped, codes, scales, sums, new_state = {}, {}, {}, {}, {}, {}, {}
+        q_unit, cos_unit, sin_unit, state_unit = {}, {}, {}, {}
+        q_turned, cos_turned, sin_turned, same, other = {}, {}, {}, {}, {}
+        rotated, grouped, codes, scales, sums, new_state = {}, {}, {}, {}, {}, {}
 
         def load(first, units):
             features = slice(first * UNIT, (first + units) * UNIT)
@@ -83,28 +119,25 @@ def tile_attention_pb_kernel(tc, Q, V, state, cos, sin, out):
             state_sb = states.tile([P, units, 2 * VALUES], BF16)
             nc.sync.dma_start(out=state_sb[:], in_=state_rows[:, first : first + units, :])
             for h in range(units):
-                words = slice(h * P, (h + 1) * P)
-                q_words[first + h] = q_sb[:].bitcast(F32)[:, :, words]
-                cos_words[first + h] = cos_sb[:].bitcast(F32)[:, :, words]
-                sin_words[first + h] = sin_sb[:].bitcast(F32)[:, :, words]
+                columns = slice(h * UNIT, (h + 1) * UNIT)
+                q_unit[first + h] = q_sb[:, :, columns]
+                cos_unit[first + h] = cos_sb[:, :, columns]
+                sin_unit[first + h] = sin_sb[:, :, columns]
                 state_unit[first + h] = state_sb[:, h, :]
 
-        def turn_words(bank, words):
+        def turn_words(bank, rows):
             for j in range(PACK):
-                nc.tensor.transpose(out=bank[:, j, :], in_=words[:, j, :], identity=identity[:])
-
-        def by_half(turned):
-            return turned.rearrange("i j (p e) -> i j e p", e=2)
+                nc.tensor.transpose(out=bank[:, j, :], in_=rows[:, j, :].bitcast(F32), identity=identity[:])
 
         def turn_q(u):
             bank = q_psum.tile([P, PACK, P], F32, name="q_bank")
-            turn_words(bank, q_words[u])
+            turn_words(bank, q_unit[u])
             q_turned[u] = turned_q.tile([P, PACK, 2 * P], BF16, name="q_turned")
-            nc.scalar.copy(out=q_turned[u][:], in_=bank[:].bitcast(BF16))
+            nc.scalar.copy(out=q_turned[u][:].bitcast(F32), in_=bank[:])
 
-        def turn_table(turned, words, u):
+        def turn_table(turned, rows, u):
             turned[u] = table_psum.tile([P, PACK, P], F32, name="table_bank")
-            turn_words(turned[u], words[u])
+            turn_words(turned[u], rows[u])
 
         def multiply_rope(u):
             q_halves = by_half(q_turned[u][:])
@@ -126,7 +159,11 @@ def tile_attention_pb_kernel(tc, Q, V, state, cos, sin, out):
             )
 
         def add_rope(u):
-            grouped[u] = quantised.tile([P, 2, P, PACK], BF16, align_bytes=64, name="grouped")
+            k, s = divmod(u, CHUNK)
+            if s == 0:
+                grouped[k] = turnstile.tile(
+                    [P, CHUNK, 2, P, PACK], BF16, name="grouped%d" % (k % 2), offset=(k % 2) * GROUPED_BYTES, align_bytes=64
+                )
             for e in (EVEN, ODD):
                 bank = rope_psum.tile([P, PACK, P], F32, name="rope_bank")
                 for j in range(PACK):
@@ -136,77 +173,118 @@ def tile_attention_pb_kernel(tc, Q, V, state, cos, sin, out):
                     nc.tensor.matmul(
                         out=bank[:, j, :], lhsT=other[u][:, j, e, :], rhs=identity[:], is_transpose=True, start=False, stop=True
                     )
-                nc.scalar.copy(out=grouped[u][:, e], in_=bank[:].rearrange("p j i -> p i j"))
+                nc.scalar.copy(out=grouped[k][:, s, e], in_=bank[:].rearrange("p j i -> p i j"))
 
-        def quantise(u):
-            codes[u] = quantised.tile([P, 2, P], U32, align_bytes=64, name="codes")
-            scales[u] = quantised.tile([P, 2, P], U8, align_bytes=64, name="scales")
+        def rope_on_gpsimd(k):
+            u = CHUNK * k + TURNED
+            q_halves = halves(q_unit[u])
+            if k < 2:
+                first = gpsimd_work.tile([P, 2, PACK, P], F32, name="gpsimd_same")
+            else:
+                first = turnstile.tile(
+                    [P, 2, PACK, P], F32, name="gpsimd_same%d" % (k % 2), offset=(k % 2) * GROUPED_BYTES, align_bytes=64
+                )
+            second = gpsimd_work.tile([P, 2, PACK, P], F32, name="gpsimd_other")
+            rotated[k] = gpsimd_work.tile([P, 2, PACK, P], F32, name="rotated")
+            nc.gpsimd.tensor_tensor(out=first[:], in0=halves(cos_unit[u]), in1=q_halves, op=MULT)
+            nc.gpsimd.tensor_tensor(out=second[:], in0=halves(sin_unit[u]), in1=q_halves[:, ::-1], op=MULT)
+            for e, combine in ((EVEN, SUBTRACT), (ODD, ADD)):
+                nc.gpsimd.tensor_tensor(out=rotated[k][:, e], in0=first[:, e], in1=second[:, e], op=combine)
+
+        def regroup(k):
+            for e in (EVEN, ODD):
+                nc.scalar.copy(out=grouped[k][:, TURNED, e], in_=rotated[k][:, e].rearrange("p j i -> p i j"))
+
+        def quantise(k):
+            codes[k] = quantised.tile([P, CHUNK, 2, P], U32, align_bytes=64, name="codes")
+            scales[k] = quantised.tile([P, CHUNK, 2, P], U8, align_bytes=64, name="scales")
             nc.vector.quantize_mx(
-                out=codes[u][:].rearrange("p e i -> p (e i)").bitcast(FP8X4),
-                scales=scales[u][:].rearrange("p e i -> p (e i)"),
-                in_=grouped[u][:].rearrange("p e i j -> p (e i j)"),
+                out=codes[k][:].rearrange("p s e i -> p (s e i)").bitcast(FP8X4),
+                scales=scales[k][:].rearrange("p s e i -> p (s e i)"),
+                in_=grouped[k][:].rearrange("p s e i j -> p (s e i j)"),
             )
 
-        def multiply(u):
-            sums[u] = sums_psum.tile([P, 2, VALUES], F32, name="sums")
-            for e in (EVEN, ODD):
-                nc.tensor.matmul_mx(
-                    out=sums[u][:, e, :],
-                    lhsT=codes[u][:, e, :].bitcast(FP8X4),
-                    lhsT_scale=scales[u][:, e, :],
-                    rhs=v_codes[:].bitcast(FP8X4),
-                    rhs_scale=v_scales[:],
-                    start=True,
-                    stop=True,
+        def multiply(k, pair):
+            for s in (2 * pair, 2 * pair + 1):
+                sums[k, s] = sums_psum.tile([P, 2, VALUES], F32, name="sums")
+                for e in (EVEN, ODD):
+                    nc.tensor.matmul_mx(
+                        out=sums[k, s][:, e, :],
+                        lhsT=codes[k][:, s, e, :].bitcast(FP8X4),
+                        lhsT_scale=scales[k][:, s, e, :],
+                        rhs=v_codes[:].bitcast(FP8X4),
+                        rhs_scale=v_scales[:],
+                        start=True,
+                        stop=True,
+                    )
+
+        def add_to_state(k, pair):
+            new_state[k, pair] = results.tile([P, 2, 2 * VALUES], F32, name="new_state")
+            for h in range(2):
+                s = 2 * pair + h
+                nc.vector.scalar_tensor_tensor(
+                    out=new_state[k, pair][:, h, :],
+                    in0=sums[k, s][:].rearrange("i e d -> i (e d)"),
+                    scalar=SCALE,
+                    in1=state_unit[CHUNK * k + s],
+                    op0=MULT,
+                    op1=ADD,
                 )
 
-        def add_to_state(u):
-            new_state[u] = results.tile([P, 2 * VALUES], F32, name="new_state")
-            nc.vector.scalar_tensor_tensor(
-                out=new_state[u][:],
-                in0=sums[u][:].rearrange("i e d -> i (e d)"),
-                scalar=SCALE,
-                in1=state_unit[u],
-                op0=MULT,
-                op1=ADD,
-            )
+        def store(k, pair):
+            first = CHUNK * k + 2 * pair
+            nc.sync.dma_start(out=out_rows[:, first : first + 2, :], in_=new_state[k, pair][:])
 
-        def store(u):
-            nc.scalar.dma_start(out=out_rows[:, u, :], in_=new_state[u][:])
-
-        first_turn = -2
         load_turn = {}
         firsts = [sum(LOAD_UNITS[:n]) for n in range(len(LOAD_UNITS))]
-        for n, first in enumerate(firsts):
-            at = max(first_turn, first - 2 - LOAD_AHEAD)
+
+        def units_of_load(n):
+            return range(firsts[n], firsts[n] + LOAD_UNITS[n])
+
+        for n in range(len(LOAD_UNITS)):
+            at = max(FIRST_TURN, min([first_use(u) for u in units_of_load(n)]) - LOAD_AHEAD)
             if n >= LOAD_BUFS:
-                at = max(at, firsts[n - LOAD_BUFS] + LOAD_UNITS[n - LOAD_BUFS] - 1)
+                at = max(at, max([last_use(u) for u in units_of_load(n - LOAD_BUFS)]) + 1)
             if n >= STATE_BUFS:
-                at = max(at, firsts[n - STATE_BUFS] + LOAD_UNITS[n - STATE_BUFS] + 3)
+                at = max(at, max([state_use(u) for u in units_of_load(n - STATE_BUFS)]) + 1)
             load_turn.setdefault(at, []).append(n)
 
-        def within(u):
-            return 0 <= u < UNITS
+        def chunk_due(turn, delay):
+            k, rest = divmod(turn - delay, TURNED)
+            return k if rest == 0 and 0 <= k < CHUNKS else None
+
+        def within(v):
+            return 0 <= v < TURNS
 
         with tc.manual_schedule():
-            for turn in range(first_turn, UNITS + 5):
+            for turn in range(FIRST_TURN, TURNS + 5):
                 for n in load_turn.get(turn, []):
                     load(firsts[n], LOAD_UNITS[n])
-                if within(turn - 4):
-                    store(turn - 4)
-                if within(turn - 3):
-                    multiply(turn - 3)
+                if chunk_due(turn, 6) is not None:
+                    store(chunk_due(turn, 6), 0)
+                if chunk_due(turn, 7) is not None:
+                    store(chunk_due(turn, 7), 1)
+                if chunk_due(turn, 2) is not None:
+                    regroup(chunk_due(turn, 2))
                 if within(turn - 1):
-                    add_rope(turn - 1)
+                    add_rope(unit_of_turn(turn - 1))
+                if chunk_due(turn, 5) is not None:
+                    multiply(chunk_due(turn, 5), 0)
+                if chunk_due(turn, 6) is not None:
+                    multiply(chunk_due(turn, 6), 1)
                 if within(turn + 1):
-                    turn_table(cos_turned, cos_words, turn + 1)
+                    turn_table(cos_turned, cos_unit, unit_of_turn(turn + 1))
                 if within(turn + 2):
-                    turn_q(turn + 2)
+                    turn_q(unit_of_turn(turn + 2))
                 if within(turn + 1):
-                    turn_table(sin_turned, sin_words, turn + 1)
+                    turn_table(sin_turned, sin_unit, unit_of_turn(turn + 1))
                 if within(turn):
-                    multiply_rope(turn)
-                if within(turn - 2):
-                    quantise(turn - 2)
-                if within(turn - 3):
-                    add_to_state(turn - 3)
+                    multiply_rope(unit_of_turn(turn))
+                if chunk_due(turn, 4) is not None:
+                    quantise(chunk_due(turn, 4))
+                if chunk_due(turn, -2) is not None:
+                    rope_on_gpsimd(chunk_due(turn, -2))
+                if chunk_due(turn, 5) is not None:
+                    add_to_state(chunk_due(turn, 5), 0)
+                if chunk_due(turn, 6) is not None:
+                    add_to_state(chunk_due(turn, 6), 1)

@@ -27,10 +27,10 @@ TURNED = CHUNK - 1
 TURNS = CHUNKS * TURNED
 EVEN, ODD = 0, 1
 GROUPED_BYTES = CHUNK * UNIT * PACK * 2
-LOAD_UNITS = (1, 1, 2) + (CHUNK,) * (CHUNKS - 1)
+LOAD_UNITS = (1, 1, 2, 2, 2) + (CHUNK,) * (CHUNKS - 2)
 assert sum(LOAD_UNITS) == UNITS
 LOAD_BUFS = 4
-STATE_BUFS = 5
+STATE_BUFS = 4
 LOAD_AHEAD = 6
 FIRST_TURN = -2
 
@@ -49,11 +49,6 @@ def first_use(u):
 def last_use(u):
     k, s = divmod(u, CHUNK)
     return TURNED * k - 2 if s == TURNED else TURNED * k + s - 1
-
-
-def state_use(u):
-    k, s = divmod(u, CHUNK)
-    return TURNED * k + 5 + s // 2
 
 
 def halves(rows):
@@ -116,14 +111,17 @@ def tile_attention_pb_kernel(tc, Q, V, state, cos, sin, out):
             nc.sync.dma_start(out=cos_sb[:], in_=cos_rows[:, :, features])
             sin_sb = loads.tile([P, PACK, units * UNIT], BF16)
             nc.sync.dma_start(out=sin_sb[:], in_=sin_rows[:, :, features])
-            state_sb = states.tile([P, units, 2 * VALUES], BF16)
-            nc.sync.dma_start(out=state_sb[:], in_=state_rows[:, first : first + units, :])
             for h in range(units):
                 columns = slice(h * UNIT, (h + 1) * UNIT)
                 q_unit[first + h] = q_sb[:, :, columns]
                 cos_unit[first + h] = cos_sb[:, :, columns]
                 sin_unit[first + h] = sin_sb[:, :, columns]
-                state_unit[first + h] = state_sb[:, h, :]
+
+        def load_state(k):
+            state_sb = states.tile([P, CHUNK, 2 * VALUES], BF16)
+            nc.sync.dma_start(out=state_sb[:], in_=state_rows[:, CHUNK * k : CHUNK * (k + 1), :])
+            for s in range(CHUNK):
+                state_unit[CHUNK * k + s] = state_sb[:, s, :]
 
         def turn_words(bank, rows):
             for j in range(PACK):
@@ -162,7 +160,7 @@ def tile_attention_pb_kernel(tc, Q, V, state, cos, sin, out):
             k, s = divmod(u, CHUNK)
             if s == 0:
                 grouped[k] = turnstile.tile(
-                    [P, CHUNK, 2, P, PACK], BF16, name="grouped%d" % (k % 2), offset=(k % 2) * GROUPED_BYTES, align_bytes=64
+                    [P, CHUNK, 2, P, PACK], BF16, name="grouped%d" % (k % 3), offset=(k % 3) * GROUPED_BYTES, align_bytes=64
                 )
             for e in (EVEN, ODD):
                 bank = rope_psum.tile([P, PACK, P], F32, name="rope_bank")
@@ -181,8 +179,9 @@ def tile_attention_pb_kernel(tc, Q, V, state, cos, sin, out):
             if k < 2:
                 first = gpsimd_work.tile([P, 2, PACK, P], F32, name="gpsimd_same")
             else:
+                place = (k - 2) % 3
                 first = turnstile.tile(
-                    [P, 2, PACK, P], F32, name="gpsimd_same%d" % (k % 2), offset=(k % 2) * GROUPED_BYTES, align_bytes=64
+                    [P, 2, PACK, P], F32, name="gpsimd_same%d" % place, offset=place * GROUPED_BYTES, align_bytes=64
                 )
             second = gpsimd_work.tile([P, 2, PACK, P], F32, name="gpsimd_other")
             rotated[k] = gpsimd_work.tile([P, 2, PACK, P], F32, name="rotated")
@@ -245,8 +244,6 @@ def tile_attention_pb_kernel(tc, Q, V, state, cos, sin, out):
             at = max(FIRST_TURN, min([first_use(u) for u in units_of_load(n)]) - LOAD_AHEAD)
             if n >= LOAD_BUFS:
                 at = max(at, max([last_use(u) for u in units_of_load(n - LOAD_BUFS)]) + 1)
-            if n >= STATE_BUFS:
-                at = max(at, max([state_use(u) for u in units_of_load(n - STATE_BUFS)]) + 1)
             load_turn.setdefault(at, []).append(n)
 
         def chunk_due(turn, delay):
@@ -260,12 +257,14 @@ def tile_attention_pb_kernel(tc, Q, V, state, cos, sin, out):
             for turn in range(FIRST_TURN, TURNS + 5):
                 for n in load_turn.get(turn, []):
                     load(firsts[n], LOAD_UNITS[n])
+                if chunk_due(turn, -1) is not None:
+                    load_state(chunk_due(turn, -1))
                 if chunk_due(turn, 6) is not None:
                     store(chunk_due(turn, 6), 0)
                 if chunk_due(turn, 7) is not None:
                     store(chunk_due(turn, 7), 1)
-                if chunk_due(turn, 2) is not None:
-                    regroup(chunk_due(turn, 2))
+                if chunk_due(turn, 3) is not None:
+                    regroup(chunk_due(turn, 3))
                 if within(turn - 1):
                     add_rope(unit_of_turn(turn - 1))
                 if chunk_due(turn, 5) is not None:

@@ -56,7 +56,7 @@ def halves(rows):
 
 
 def by_half(turned):
-    return turned.rearrange("i j (p e) -> i j e p", e=2)
+    return turned.rearrange("i j (p e) -> i e (j p)", e=2)
 
 
 def tile_attention_pb_kernel(tc, Q, V, state, cos, sin, out):
@@ -141,19 +141,21 @@ def tile_attention_pb_kernel(tc, Q, V, state, cos, sin, out):
             q_halves = by_half(q_turned[u][:])
             cos_halves = by_half(cos_turned[u][:].bitcast(BF16))
             sin_halves = by_half(sin_turned[u][:].bitcast(BF16))
-            same[u] = products.tile([P, PACK, 2, P], F32, name="same")
-            other[u] = products.tile([P, PACK, 2, P], F32, name="other")
-            nc.vector.tensor_tensor(out=same[u][:], in0=cos_halves, in1=q_halves, op=MULT)
+            same[u] = products.tile([P, 2, PACK, P], F32, name="same")
+            other[u] = products.tile([P, 2, PACK, P], F32, name="other")
+            nc.vector.tensor_tensor(
+                out=same[u][:].rearrange("i e j p -> i e (j p)"), in0=cos_halves, in1=q_halves, op=MULT
+            )
             nc.vector.scalar_tensor_tensor(
-                out=other[u][:, :, EVEN, :],
-                in0=sin_halves[:, :, EVEN, :],
+                out=other[u][:, EVEN].rearrange("i j p -> i (j p)"),
+                in0=sin_halves[:, EVEN],
                 scalar=-1.0,
-                in1=q_halves[:, :, ODD, :],
+                in1=q_halves[:, ODD],
                 op0=MULT,
                 op1=MULT,
             )
             nc.vector.tensor_tensor(
-                out=other[u][:, :, ODD, :], in0=sin_halves[:, :, ODD, :], in1=q_halves[:, :, EVEN, :], op=MULT
+                out=other[u][:, ODD].rearrange("i j p -> i (j p)"), in0=sin_halves[:, ODD], in1=q_halves[:, EVEN], op=MULT
             )
 
         def add_rope(u):
@@ -166,10 +168,10 @@ def tile_attention_pb_kernel(tc, Q, V, state, cos, sin, out):
                 bank = rope_psum.tile([P, PACK, P], F32, name="rope_bank")
                 for j in range(PACK):
                     nc.tensor.matmul(
-                        out=bank[:, j, :], lhsT=same[u][:, j, e, :], rhs=identity[:], is_transpose=True, start=True, stop=False
+                        out=bank[:, j, :], lhsT=same[u][:, e, j, :], rhs=identity[:], is_transpose=True, start=True, stop=False
                     )
                     nc.tensor.matmul(
-                        out=bank[:, j, :], lhsT=other[u][:, j, e, :], rhs=identity[:], is_transpose=True, start=False, stop=True
+                        out=bank[:, j, :], lhsT=other[u][:, e, j, :], rhs=identity[:], is_transpose=True, start=False, stop=True
                     )
                 nc.scalar.copy(out=grouped[k][:, s, e], in_=bank[:].rearrange("p j i -> p i j"))
 

@@ -133,8 +133,10 @@ def tile_attention_pb_kernel(tc, Q, V, state, cos, sin, out):
             q_turned[u] = turned_q.tile([P, PACK, 2 * P], BF16, name="q_turned")
             nc.scalar.copy(out=q_turned[u][:].bitcast(F32), in_=bank[:])
 
-        def turn_table(turned, rows, u):
+        def turn_table(turned, rows, u, idle):
             turned[u] = table_psum.tile([P, PACK, P], F32, name="table_bank")
+            if idle:
+                hold_clock(turned[u])
             turn_words(turned[u], rows[u])
 
         def multiply_rope(u):
@@ -158,7 +160,7 @@ def tile_attention_pb_kernel(tc, Q, V, state, cos, sin, out):
                 out=other[u][:, ODD].rearrange("i j p -> i (j p)"), in0=sin_halves[:, ODD], in1=q_halves[:, EVEN], op=MULT
             )
 
-        def add_rope(u):
+        def add_rope(u, idle):
             k, s = divmod(u, CHUNK)
             if s == 0:
                 grouped[k] = turnstile.tile(
@@ -166,6 +168,8 @@ def tile_attention_pb_kernel(tc, Q, V, state, cos, sin, out):
                 )
             for e in (EVEN, ODD):
                 bank = rope_psum.tile([P, PACK, P], F32, name="rope_bank")
+                if idle and e == EVEN:
+                    hold_clock(bank)
                 for j in range(PACK):
                     nc.tensor.matmul(
                         out=bank[:, j, :], lhsT=same[u][:, e, j, :], rhs=identity[:], is_transpose=True, start=True, stop=False
@@ -196,17 +200,19 @@ def tile_attention_pb_kernel(tc, Q, V, state, cos, sin, out):
             for e in (EVEN, ODD):
                 nc.scalar.copy(out=grouped[k][:, TURNED, e], in_=rotated[k][:, e].rearrange("p j i -> p i j"))
 
-        def quantise(k):
-            codes[k] = quantised.tile([P, CHUNK, 2, P], U32, align_bytes=64, name="codes")
-            scales[k] = quantised.tile([P, CHUNK, 2, P], U8, align_bytes=64, name="scales")
+        def quantise(k, first, units):
+            if first == 0:
+                codes[k] = quantised.tile([P, CHUNK, 2, P], U32, align_bytes=64, name="codes")
+                scales[k] = quantised.tile([P, CHUNK, 2, P], U8, align_bytes=64, name="scales")
+            part = slice(first, first + units)
             nc.vector.quantize_mx(
-                out=codes[k][:].rearrange("p s e i -> p (s e i)").bitcast(FP8X4),
-                scales=scales[k][:].rearrange("p s e i -> p (s e i)"),
-                in_=grouped[k][:].rearrange("p s e i j -> p (s e i j)"),
+                out=codes[k][:, part].rearrange("p s e i -> p (s e i)").bitcast(FP8X4),
+                scales=scales[k][:, part].rearrange("p s e i -> p (s e i)"),
+                in_=grouped[k][:, part].rearrange("p s e i j -> p (s e i j)"),
             )
 
-        def multiply(k, pair):
-            for s in (2 * pair, 2 * pair + 1):
+        def multiply(k, units):
+            for s in units:
                 sums[k, s] = sums_psum.tile([P, 2, VALUES], F32, name="sums")
                 for e in (EVEN, ODD):
                     nc.tensor.matmul_mx(
@@ -218,6 +224,19 @@ def tile_attention_pb_kernel(tc, Q, V, state, cos, sin, out):
                         start=True,
                         stop=True,
                     )
+
+        def hold_clock(bank):
+            columns = bank[:].rearrange("p j i -> p (j i)")
+            for h in range(2):
+                nc.tensor.matmul_mx(
+                    out=columns[:, h * VALUES : (h + 1) * VALUES],
+                    lhsT=v_codes[:, :P].bitcast(FP8X4),
+                    lhsT_scale=v_scales[:, :P],
+                    rhs=v_codes[:].bitcast(FP8X4),
+                    rhs_scale=v_scales[:],
+                    start=True,
+                    stop=True,
+                )
 
         def add_to_state(k, pair):
             new_state[k, pair] = results.tile([P, 2, 2 * VALUES], F32, name="new_state")
@@ -248,44 +267,63 @@ def tile_attention_pb_kernel(tc, Q, V, state, cos, sin, out):
                 at = max(at, max([last_use(u) for u in units_of_load(n - LOAD_BUFS)]) + 1)
             load_turn.setdefault(at, []).append(n)
 
-        def chunk_due(turn, delay):
+        LAST = CHUNKS - 1
+
+        def chunk_due(turn, delay, last_delay):
+            if turn - last_delay == TURNED * LAST:
+                return LAST
             k, rest = divmod(turn - delay, TURNED)
-            return k if rest == 0 and 0 <= k < CHUNKS else None
+            return k if rest == 0 and 0 <= k < LAST else None
 
         def within(v):
             return 0 <= v < TURNS
 
         with tc.manual_schedule():
-            for turn in range(FIRST_TURN, TURNS + 5):
+            passes_before = False
+            for turn in range(FIRST_TURN, TURNS + 4):
                 for n in load_turn.get(turn, []):
                     load(firsts[n], LOAD_UNITS[n])
-                if chunk_due(turn, -1) is not None:
-                    load_state(chunk_due(turn, -1))
-                if chunk_due(turn, 6) is not None:
-                    store(chunk_due(turn, 6), 0)
-                if chunk_due(turn, 7) is not None:
-                    store(chunk_due(turn, 7), 1)
-                if chunk_due(turn, 3) is not None:
-                    regroup(chunk_due(turn, 3))
+                if chunk_due(turn, -1, -1) is not None:
+                    load_state(chunk_due(turn, -1, -1))
+                if chunk_due(turn, 6, 5) is not None:
+                    store(chunk_due(turn, 6, 5), 0)
+                if chunk_due(turn, 7, 6) is not None:
+                    store(chunk_due(turn, 7, 6), 1)
+                if chunk_due(turn, 3, 3) is not None:
+                    regroup(chunk_due(turn, 3, 3))
+                first_pair, second_pair = chunk_due(turn, 5, 4), chunk_due(turn, 6, 5)
                 if within(turn - 1):
-                    add_rope(unit_of_turn(turn - 1))
-                if chunk_due(turn, 5) is not None:
-                    multiply(chunk_due(turn, 5), 0)
-                if chunk_due(turn, 6) is not None:
-                    multiply(chunk_due(turn, 6), 1)
+                    add_rope(unit_of_turn(turn - 1), not passes_before)
+                if first_pair == LAST or second_pair == LAST:
+                    multiply(LAST, (0, 1) if first_pair == LAST else (2, 3))
+                elif first_pair is not None:
+                    multiply(first_pair, (0,))
+                elif second_pair is not None:
+                    multiply(second_pair, (2,))
                 if within(turn + 1):
-                    turn_table(cos_turned, cos_unit, unit_of_turn(turn + 1))
+                    turn_table(cos_turned, cos_unit, unit_of_turn(turn + 1), first_pair is None and second_pair is None)
                 if within(turn + 2):
                     turn_q(unit_of_turn(turn + 2))
                 if within(turn + 1):
-                    turn_table(sin_turned, sin_unit, unit_of_turn(turn + 1))
+                    turn_table(sin_turned, sin_unit, unit_of_turn(turn + 1), False)
+                passes_before = False
+                if first_pair is not None and first_pair != LAST:
+                    multiply(first_pair, (1,))
+                    passes_before = True
+                elif second_pair is not None and second_pair != LAST:
+                    multiply(second_pair, (3,))
+                    passes_before = True
                 if within(turn):
                     multiply_rope(unit_of_turn(turn))
-                if chunk_due(turn, 4) is not None:
-                    quantise(chunk_due(turn, 4))
-                if chunk_due(turn, -2) is not None:
-                    rope_on_gpsimd(chunk_due(turn, -2))
-                if chunk_due(turn, 5) is not None:
-                    add_to_state(chunk_due(turn, 5), 0)
-                if chunk_due(turn, 6) is not None:
-                    add_to_state(chunk_due(turn, 6), 1)
+                if turn == TURNED * LAST + 3:
+                    quantise(LAST, 0, 2)
+                elif turn == TURNED * LAST + 4:
+                    quantise(LAST, 2, 2)
+                elif chunk_due(turn, 4, 4) is not None:
+                    quantise(chunk_due(turn, 4, 4), 0, CHUNK)
+                if chunk_due(turn, -2, -2) is not None:
+                    rope_on_gpsimd(chunk_due(turn, -2, -2))
+                if chunk_due(turn, 5, 4) is not None:
+                    add_to_state(chunk_due(turn, 5, 4), 0)
+                if chunk_due(turn, 6, 5) is not None:
+                    add_to_state(chunk_due(turn, 6, 5), 1)

@@ -32,6 +32,8 @@ assert sum(LOAD_UNITS) == UNITS
 LOAD_BUFS = 4
 STATE_BUFS = 4
 LOAD_AHEAD = 6
+RESULT_BUFS = 8
+STORE_TURNS = 3
 FIRST_TURN = -2
 
 FLOPS = 2 * TOKENS * FEATURES * VALUES
@@ -78,7 +80,7 @@ def tile_attention_pb_kernel(tc, Q, V, state, cos, sin, out):
         turnstile = ctx.enter_context(tc.tile_pool(name="turnstile", bufs=1))
         gpsimd_work = ctx.enter_context(tc.tile_pool(name="gpsimd_work", bufs=2))
         quantised = ctx.enter_context(tc.tile_pool(name="quantised", bufs=2))
-        results = ctx.enter_context(tc.tile_pool(name="results", bufs=3))
+        results = ctx.enter_context(tc.tile_pool(name="results", bufs=RESULT_BUFS))
         q_psum = ctx.enter_context(tc.psum_pool(name="q_psum", bufs=1))
         table_psum = ctx.enter_context(tc.psum_pool(name="table_psum", bufs=3))
         rope_psum = ctx.enter_context(tc.psum_pool(name="rope_psum", bufs=2))
@@ -133,10 +135,8 @@ def tile_attention_pb_kernel(tc, Q, V, state, cos, sin, out):
             q_turned[u] = turned_q.tile([P, PACK, 2 * P], BF16, name="q_turned")
             nc.scalar.copy(out=q_turned[u][:].bitcast(F32), in_=bank[:])
 
-        def turn_table(turned, rows, u, idle):
+        def turn_table(turned, rows, u):
             turned[u] = table_psum.tile([P, PACK, P], F32, name="table_bank")
-            if idle:
-                hold_clock(turned[u])
             turn_words(turned[u], rows[u])
 
         def multiply_rope(u):
@@ -160,7 +160,7 @@ def tile_attention_pb_kernel(tc, Q, V, state, cos, sin, out):
                 out=other[u][:, ODD].rearrange("i j p -> i (j p)"), in0=sin_halves[:, ODD], in1=q_halves[:, EVEN], op=MULT
             )
 
-        def add_rope(u, idle):
+        def add_rope(u):
             k, s = divmod(u, CHUNK)
             if s == 0:
                 grouped[k] = turnstile.tile(
@@ -168,8 +168,6 @@ def tile_attention_pb_kernel(tc, Q, V, state, cos, sin, out):
                 )
             for e in (EVEN, ODD):
                 bank = rope_psum.tile([P, PACK, P], F32, name="rope_bank")
-                if idle and e == EVEN:
-                    hold_clock(bank)
                 for j in range(PACK):
                     nc.tensor.matmul(
                         out=bank[:, j, :], lhsT=same[u][:, e, j, :], rhs=identity[:], is_transpose=True, start=True, stop=False
@@ -182,13 +180,10 @@ def tile_attention_pb_kernel(tc, Q, V, state, cos, sin, out):
         def rope_on_gpsimd(k):
             u = CHUNK * k + TURNED
             q_halves = halves(q_unit[u])
-            if k < 2:
-                first = gpsimd_work.tile([P, 2, PACK, P], F32, name="gpsimd_same")
-            else:
-                place = (k - 2) % 3
-                first = turnstile.tile(
-                    [P, 2, PACK, P], F32, name="gpsimd_same%d" % place, offset=place * GROUPED_BYTES, align_bytes=64
-                )
+            place = (k - 2) % 3
+            first = turnstile.tile(
+                [P, 2, PACK, P], F32, name="gpsimd_same%d" % place, offset=place * GROUPED_BYTES, align_bytes=64
+            )
             second = gpsimd_work.tile([P, 2, PACK, P], F32, name="gpsimd_other")
             rotated[k] = gpsimd_work.tile([P, 2, PACK, P], F32, name="rotated")
             nc.gpsimd.tensor_tensor(out=first[:], in0=halves(cos_unit[u]), in1=q_halves, op=MULT)
@@ -211,8 +206,8 @@ def tile_attention_pb_kernel(tc, Q, V, state, cos, sin, out):
                 in_=grouped[k][:, part].rearrange("p s e i j -> p (s e i j)"),
             )
 
-        def multiply(k, units):
-            for s in units:
+        def multiply(k, pair):
+            for s in (2 * pair, 2 * pair + 1):
                 sums[k, s] = sums_psum.tile([P, 2, VALUES], F32, name="sums")
                 for e in (EVEN, ODD):
                     nc.tensor.matmul_mx(
@@ -224,19 +219,6 @@ def tile_attention_pb_kernel(tc, Q, V, state, cos, sin, out):
                         start=True,
                         stop=True,
                     )
-
-        def hold_clock(bank):
-            columns = bank[:].rearrange("p j i -> p (j i)")
-            for h in range(2):
-                nc.tensor.matmul_mx(
-                    out=columns[:, h * VALUES : (h + 1) * VALUES],
-                    lhsT=v_codes[:, :P].bitcast(FP8X4),
-                    lhsT_scale=v_scales[:, :P],
-                    rhs=v_codes[:].bitcast(FP8X4),
-                    rhs_scale=v_scales[:],
-                    start=True,
-                    stop=True,
-                )
 
         def add_to_state(k, pair):
             new_state[k, pair] = results.tile([P, 2, 2 * VALUES], F32, name="new_state")
@@ -269,6 +251,14 @@ def tile_attention_pb_kernel(tc, Q, V, state, cos, sin, out):
 
         LAST = CHUNKS - 1
 
+        store_turn = {}
+        last_load = max(load_turn)
+        for k in range(CHUNKS):
+            for pair in range(2):
+                added = TURNED * k + pair + (4 if k == LAST else 5)
+                latest = added + TURNED * RESULT_BUFS // 2 - STORE_TURNS
+                store_turn.setdefault(min(latest, max(added + 1, last_load)), []).append((k, pair))
+
         def chunk_due(turn, delay, last_delay):
             if turn - last_delay == TURNED * LAST:
                 return LAST
@@ -279,40 +269,27 @@ def tile_attention_pb_kernel(tc, Q, V, state, cos, sin, out):
             return 0 <= v < TURNS
 
         with tc.manual_schedule():
-            passes_before = False
             for turn in range(FIRST_TURN, TURNS + 4):
                 for n in load_turn.get(turn, []):
                     load(firsts[n], LOAD_UNITS[n])
                 if chunk_due(turn, -1, -1) is not None:
                     load_state(chunk_due(turn, -1, -1))
-                if chunk_due(turn, 6, 5) is not None:
-                    store(chunk_due(turn, 6, 5), 0)
-                if chunk_due(turn, 7, 6) is not None:
-                    store(chunk_due(turn, 7, 6), 1)
+                for k, pair in store_turn.get(turn, []):
+                    store(k, pair)
                 if chunk_due(turn, 3, 3) is not None:
                     regroup(chunk_due(turn, 3, 3))
-                first_pair, second_pair = chunk_due(turn, 5, 4), chunk_due(turn, 6, 5)
                 if within(turn - 1):
-                    add_rope(unit_of_turn(turn - 1), not passes_before)
-                if first_pair == LAST or second_pair == LAST:
-                    multiply(LAST, (0, 1) if first_pair == LAST else (2, 3))
-                elif first_pair is not None:
-                    multiply(first_pair, (0,))
-                elif second_pair is not None:
-                    multiply(second_pair, (2,))
+                    add_rope(unit_of_turn(turn - 1))
+                if chunk_due(turn, 5, 4) is not None:
+                    multiply(chunk_due(turn, 5, 4), 0)
+                if chunk_due(turn, 6, 5) is not None:
+                    multiply(chunk_due(turn, 6, 5), 1)
                 if within(turn + 1):
-                    turn_table(cos_turned, cos_unit, unit_of_turn(turn + 1), first_pair is None and second_pair is None)
+                    turn_table(cos_turned, cos_unit, unit_of_turn(turn + 1))
                 if within(turn + 2):
                     turn_q(unit_of_turn(turn + 2))
                 if within(turn + 1):
-                    turn_table(sin_turned, sin_unit, unit_of_turn(turn + 1), False)
-                passes_before = False
-                if first_pair is not None and first_pair != LAST:
-                    multiply(first_pair, (1,))
-                    passes_before = True
-                elif second_pair is not None and second_pair != LAST:
-                    multiply(second_pair, (3,))
-                    passes_before = True
+                    turn_table(sin_turned, sin_unit, unit_of_turn(turn + 1))
                 if within(turn):
                     multiply_rope(unit_of_turn(turn))
                 if turn == TURNED * LAST + 3:

@@ -26,13 +26,17 @@ CHUNKS = UNITS // CHUNK
 TURNED = CHUNK - 1
 TURNS = CHUNKS * TURNED
 EVEN, ODD = 0, 1
+GROUP = 2
+GROUPS = CHUNK // GROUP
+ROWS = 2 * GROUP
+BANKS = CHUNK
 GROUPED_BYTES = CHUNK * UNIT * PACK * 2
-LOAD_UNITS = (1, 1, 2, 2, 2) + (CHUNK,) * (CHUNKS - 2)
+LOAD_UNITS = (CHUNK,) * CHUNKS
 assert sum(LOAD_UNITS) == UNITS
 LOAD_BUFS = 4
 STATE_BUFS = 4
 LOAD_AHEAD = 6
-RESULT_BUFS = 8
+RESULT_BUFS = 9
 STORE_TURNS = 3
 FIRST_TURN = -2
 
@@ -61,6 +65,10 @@ def by_half(turned):
     return turned.rearrange("i j (p e) -> i e (j p)", e=2)
 
 
+def by_parity(sums):
+    return sums.rearrange("p j (m parity) -> p parity m j", parity=2)
+
+
 def tile_attention_pb_kernel(tc, Q, V, state, cos, sin, out):
     nc = tc.nc
 
@@ -68,8 +76,8 @@ def tile_attention_pb_kernel(tc, Q, V, state, cos, sin, out):
     cos_rows = cos.rearrange("(p j) f -> p j f", j=PACK)
     sin_rows = sin.rearrange("(p j) f -> p j f", j=PACK)
     v_rows = V.flatten_outer_dims().rearrange("(p j) d -> p j d", j=PACK)
-    state_rows = state.flatten_outer_dims().rearrange("(n i e) d -> i n (e d)", i=P, e=2)
-    out_rows = out.flatten_outer_dims().rearrange("(n i e) d -> i n (e d)", i=P, e=2)
+    state_rows = state.flatten_outer_dims().rearrange("(n i r) d -> i n (r d)", i=P, r=ROWS)
+    out_rows = out.flatten_outer_dims().rearrange("(n i r) d -> i n (r d)", i=P, r=ROWS)
 
     with ExitStack() as ctx:
         keep = ctx.enter_context(tc.tile_pool(name="keep", bufs=1))
@@ -101,7 +109,7 @@ def tile_attention_pb_kernel(tc, Q, V, state, cos, sin, out):
             in_=v_grouped[:].rearrange("p d j -> p (d j)"),
         )
 
-        q_unit, cos_unit, sin_unit, state_unit = {}, {}, {}, {}
+        q_unit, cos_unit, sin_unit, state_bank = {}, {}, {}, {}
         q_turned, cos_turned, sin_turned, same, other = {}, {}, {}, {}, {}
         rotated, grouped, codes, scales, sums, new_state = {}, {}, {}, {}, {}, {}
 
@@ -120,10 +128,10 @@ def tile_attention_pb_kernel(tc, Q, V, state, cos, sin, out):
                 sin_unit[first + h] = sin_sb[:, :, columns]
 
         def load_state(k):
-            state_sb = states.tile([P, CHUNK, 2 * VALUES], BF16)
-            nc.sync.dma_start(out=state_sb[:], in_=state_rows[:, CHUNK * k : CHUNK * (k + 1), :])
-            for s in range(CHUNK):
-                state_unit[CHUNK * k + s] = state_sb[:, s, :]
+            state_sb = states.tile([P, GROUPS, ROWS * VALUES], BF16)
+            nc.sync.dma_start(out=state_sb[:], in_=state_rows[:, GROUPS * k : GROUPS * (k + 1), :])
+            for b in range(BANKS):
+                state_bank[k, b] = state_sb[:].rearrange("i g (h c) -> i (g h) c", h=2)[:, b, :]
 
         def turn_words(bank, rows):
             for j in range(PACK):
@@ -160,11 +168,15 @@ def tile_attention_pb_kernel(tc, Q, V, state, cos, sin, out):
                 out=other[u][:, ODD].rearrange("i j p -> i (j p)"), in0=sin_halves[:, ODD], in1=q_halves[:, EVEN], op=MULT
             )
 
+        def place_in_grouped(k, s, e):
+            g, half = divmod(s, GROUP)
+            return grouped[k][:, g, e::2, half * (P // 2) : (half + 1) * (P // 2), :]
+
         def add_rope(u):
             k, s = divmod(u, CHUNK)
             if s == 0:
                 grouped[k] = turnstile.tile(
-                    [P, CHUNK, 2, P, PACK], BF16, name="grouped%d" % (k % 3), offset=(k % 3) * GROUPED_BYTES, align_bytes=64
+                    [P, GROUPS, ROWS, P, PACK], BF16, name="grouped%d" % (k % 3), offset=(k % 3) * GROUPED_BYTES, align_bytes=64
                 )
             for e in (EVEN, ODD):
                 bank = rope_psum.tile([P, PACK, P], F32, name="rope_bank")
@@ -175,7 +187,7 @@ def tile_attention_pb_kernel(tc, Q, V, state, cos, sin, out):
                     nc.tensor.matmul(
                         out=bank[:, j, :], lhsT=other[u][:, e, j, :], rhs=identity[:], is_transpose=True, start=False, stop=True
                     )
-                nc.scalar.copy(out=grouped[k][:, s, e], in_=bank[:].rearrange("p j i -> p i j"))
+                nc.scalar.copy(out=place_in_grouped(k, s, e), in_=by_parity(bank[:]))
 
         def rope_on_gpsimd(k):
             u = CHUNK * k + TURNED
@@ -193,27 +205,28 @@ def tile_attention_pb_kernel(tc, Q, V, state, cos, sin, out):
 
         def regroup(k):
             for e in (EVEN, ODD):
-                nc.scalar.copy(out=grouped[k][:, TURNED, e], in_=rotated[k][:, e].rearrange("p j i -> p i j"))
+                nc.scalar.copy(out=place_in_grouped(k, TURNED, e), in_=by_parity(rotated[k][:, e]))
 
-        def quantise(k, first, units):
+        def quantise(k, first, groups):
             if first == 0:
-                codes[k] = quantised.tile([P, CHUNK, 2, P], U32, align_bytes=64, name="codes")
-                scales[k] = quantised.tile([P, CHUNK, 2, P], U8, align_bytes=64, name="scales")
-            part = slice(first, first + units)
+                codes[k] = quantised.tile([P, GROUPS, ROWS, P], U32, align_bytes=64, name="codes")
+                scales[k] = quantised.tile([P, GROUPS, ROWS, P], U8, align_bytes=64, name="scales")
+            part = slice(first, first + groups)
             nc.vector.quantize_mx(
-                out=codes[k][:, part].rearrange("p s e i -> p (s e i)").bitcast(FP8X4),
-                scales=scales[k][:, part].rearrange("p s e i -> p (s e i)"),
-                in_=grouped[k][:, part].rearrange("p s e i j -> p (s e i j)"),
+                out=codes[k][:, part].rearrange("p g r i -> p (g r i)").bitcast(FP8X4),
+                scales=scales[k][:, part].rearrange("p g r i -> p (g r i)"),
+                in_=grouped[k][:, part].rearrange("p g r i j -> p (g r i j)"),
             )
 
-        def multiply(k, pair):
-            for s in (2 * pair, 2 * pair + 1):
+        def multiply(k, g):
+            for h in range(2):
+                s = 2 * g + h
                 sums[k, s] = sums_psum.tile([P, 2, VALUES], F32, name="sums")
-                for e in (EVEN, ODD):
+                for e in range(2):
                     nc.tensor.matmul_mx(
                         out=sums[k, s][:, e, :],
-                        lhsT=codes[k][:, s, e, :].bitcast(FP8X4),
-                        lhsT_scale=scales[k][:, s, e, :],
+                        lhsT=codes[k][:, g, 2 * h + e, :].bitcast(FP8X4),
+                        lhsT_scale=scales[k][:, g, 2 * h + e, :],
                         rhs=v_codes[:].bitcast(FP8X4),
                         rhs_scale=v_scales[:],
                         start=True,
@@ -228,14 +241,19 @@ def tile_attention_pb_kernel(tc, Q, V, state, cos, sin, out):
                     out=new_state[k, pair][:, h, :],
                     in0=sums[k, s][:].rearrange("i e d -> i (e d)"),
                     scalar=SCALE,
-                    in1=state_unit[CHUNK * k + s],
+                    in1=state_bank[k, s],
                     op0=MULT,
                     op1=ADD,
                 )
 
-        def store(k, pair):
-            first = CHUNK * k + 2 * pair
-            nc.sync.dma_start(out=out_rows[:, first : first + 2, :], in_=new_state[k, pair][:])
+        def store(k, pair, pieces):
+            width = ROWS * VALUES // pieces
+            for n in range(pieces):
+                columns = slice(n * width, (n + 1) * width)
+                nc.sync.dma_start(
+                    out=out_rows[:, GROUPS * k + pair, columns],
+                    in_=new_state[k, pair][:].rearrange("i h c -> i (h c)")[:, columns],
+                )
 
         load_turn = {}
         firsts = [sum(LOAD_UNITS[:n]) for n in range(len(LOAD_UNITS))]
@@ -275,7 +293,7 @@ def tile_attention_pb_kernel(tc, Q, V, state, cos, sin, out):
                 if chunk_due(turn, -1, -1) is not None:
                     load_state(chunk_due(turn, -1, -1))
                 for k, pair in store_turn.get(turn, []):
-                    store(k, pair)
+                    store(k, pair, 2 if (k, pair) == (LAST, 1) else 1)
                 if chunk_due(turn, 3, 3) is not None:
                     regroup(chunk_due(turn, 3, 3))
                 if within(turn - 1):
@@ -293,11 +311,11 @@ def tile_attention_pb_kernel(tc, Q, V, state, cos, sin, out):
                 if within(turn):
                     multiply_rope(unit_of_turn(turn))
                 if turn == TURNED * LAST + 3:
-                    quantise(LAST, 0, 2)
+                    quantise(LAST, 0, 1)
                 elif turn == TURNED * LAST + 4:
-                    quantise(LAST, 2, 2)
+                    quantise(LAST, 1, 1)
                 elif chunk_due(turn, 4, 4) is not None:
-                    quantise(chunk_due(turn, 4, 4), 0, CHUNK)
+                    quantise(chunk_due(turn, 4, 4), 0, GROUPS)
                 if chunk_due(turn, -2, -2) is not None:
                     rope_on_gpsimd(chunk_due(turn, -2, -2))
                 if chunk_due(turn, 5, 4) is not None:

@@ -36,9 +36,10 @@ assert sum(LOAD_UNITS) == UNITS
 LOAD_BUFS = 4
 STATE_BUFS = 4
 LOAD_AHEAD = 6
-RESULT_BUFS = 9
+RESULT_BUFS = 10
 STORE_TURNS = 3
 FIRST_TURN = -2
+TENSOR_ADDS = [(k, 3) for k in range(CHUNKS - 2)]
 
 FLOPS = 2 * TOKENS * FEATURES * VALUES
 
@@ -83,11 +84,12 @@ def tile_attention_pb_kernel(tc, Q, V, state, cos, sin, out):
         keep = ctx.enter_context(tc.tile_pool(name="keep", bufs=1))
         loads = ctx.enter_context(tc.tile_pool(name="loads", bufs=LOAD_BUFS))
         states = ctx.enter_context(tc.tile_pool(name="states", bufs=STATE_BUFS))
-        turned_q = ctx.enter_context(tc.tile_pool(name="turned_q", bufs=4))
-        products = ctx.enter_context(tc.tile_pool(name="products", bufs=3))
+        turned_q = ctx.enter_context(tc.tile_pool(name="turned_q", bufs=3))
+        products = ctx.enter_context(tc.tile_pool(name="products", bufs=2))
         turnstile = ctx.enter_context(tc.tile_pool(name="turnstile", bufs=1))
         gpsimd_work = ctx.enter_context(tc.tile_pool(name="gpsimd_work", bufs=2))
         quantised = ctx.enter_context(tc.tile_pool(name="quantised", bufs=2))
+        scaled_sums = ctx.enter_context(tc.tile_pool(name="scaled_sums", bufs=1))
         results = ctx.enter_context(tc.tile_pool(name="results", bufs=RESULT_BUFS))
         q_psum = ctx.enter_context(tc.psum_pool(name="q_psum", bufs=1))
         table_psum = ctx.enter_context(tc.psum_pool(name="table_psum", bufs=3))
@@ -96,6 +98,8 @@ def tile_attention_pb_kernel(tc, Q, V, state, cos, sin, out):
 
         identity = keep.tile([P, P], F32)
         make_identity(nc, identity[:])
+        identity_bf16 = keep.tile([P, P], BF16)
+        make_identity(nc, identity_bf16[:])
 
         v_raw = keep.tile([P, PACK, VALUES], BF16)
         nc.scalar.dma_start(out=v_raw[:], in_=v_rows)
@@ -111,7 +115,7 @@ def tile_attention_pb_kernel(tc, Q, V, state, cos, sin, out):
 
         q_unit, cos_unit, sin_unit, state_bank = {}, {}, {}, {}
         q_turned, cos_turned, sin_turned, same, other = {}, {}, {}, {}, {}
-        rotated, grouped, codes, scales, sums, new_state = {}, {}, {}, {}, {}, {}
+        rotated, grouped, codes, scales, sums, new_state, scaled = {}, {}, {}, {}, {}, {}, {}
 
         def load(first, units):
             features = slice(first * UNIT, (first + units) * UNIT)
@@ -140,15 +144,22 @@ def tile_attention_pb_kernel(tc, Q, V, state, cos, sin, out):
         def turn_q(u):
             bank = q_psum.tile([P, PACK, P], F32, name="q_bank")
             turn_words(bank, q_unit[u])
-            q_turned[u] = turned_q.tile([P, PACK, 2 * P], BF16, name="q_turned")
-            nc.scalar.copy(out=q_turned[u][:].bitcast(F32), in_=bank[:])
+            q_turned[u] = turned_q.tile([P, 2, 2 * PACK * P], BF16, name="q_turned")
+            nc.scalar.copy(out=q_turned[u][:, 1].bitcast(F32), in_=bank[:].rearrange("i j p -> i (j p)"))
+            nc.scalar.mul(
+                q_turned[u][:, 0].rearrange("i (n e) -> i e n", e=2)[:, 0],
+                bank[:].bitcast(BF16).rearrange("i j (p e) -> i e j p", e=2)[:, ODD].rearrange("i j p -> i (j p)"),
+                -1.0,
+            )
 
         def turn_table(turned, rows, u):
             turned[u] = table_psum.tile([P, PACK, P], F32, name="table_bank")
             turn_words(turned[u], rows[u])
 
         def multiply_rope(u):
-            q_halves = by_half(q_turned[u][:])
+            pairs = q_turned[u][:].rearrange("i k (n e) -> i k e n", e=2)
+            q_halves = pairs[:, 1]
+            q_crossed = pairs[:, :, EVEN]
             cos_halves = by_half(cos_turned[u][:].bitcast(BF16))
             sin_halves = by_half(sin_turned[u][:].bitcast(BF16))
             same[u] = products.tile([P, 2, PACK, P], F32, name="same")
@@ -156,16 +167,8 @@ def tile_attention_pb_kernel(tc, Q, V, state, cos, sin, out):
             nc.vector.tensor_tensor(
                 out=same[u][:].rearrange("i e j p -> i e (j p)"), in0=cos_halves, in1=q_halves, op=MULT
             )
-            nc.vector.scalar_tensor_tensor(
-                out=other[u][:, EVEN].rearrange("i j p -> i (j p)"),
-                in0=sin_halves[:, EVEN],
-                scalar=-1.0,
-                in1=q_halves[:, ODD],
-                op0=MULT,
-                op1=MULT,
-            )
             nc.vector.tensor_tensor(
-                out=other[u][:, ODD].rearrange("i j p -> i (j p)"), in0=sin_halves[:, ODD], in1=q_halves[:, EVEN], op=MULT
+                out=other[u][:].rearrange("i e j p -> i e (j p)"), in0=sin_halves, in1=q_crossed, op=MULT
             )
 
         def place_in_grouped(k, s, e):
@@ -196,7 +199,7 @@ def tile_attention_pb_kernel(tc, Q, V, state, cos, sin, out):
             first = turnstile.tile(
                 [P, 2, PACK, P], F32, name="gpsimd_same%d" % place, offset=place * GROUPED_BYTES, align_bytes=64
             )
-            second = gpsimd_work.tile([P, 2, PACK, P], F32, name="gpsimd_other")
+            second = gpsimd_work.tile([P, 2, PACK, P], F32, name="gpsimd_other", bufs=1)
             rotated[k] = gpsimd_work.tile([P, 2, PACK, P], F32, name="rotated")
             nc.gpsimd.tensor_tensor(out=first[:], in0=halves(cos_unit[u]), in1=q_halves, op=MULT)
             nc.gpsimd.tensor_tensor(out=second[:], in0=halves(sin_unit[u]), in1=q_halves[:, ::-1], op=MULT)
@@ -218,9 +221,44 @@ def tile_attention_pb_kernel(tc, Q, V, state, cos, sin, out):
                 in_=grouped[k][:, part].rearrange("p g r i j -> p (g r i j)"),
             )
 
+        def multiply_turned(k, s):
+            g, h = divmod(s, 2)
+            bank = sums_psum.tile([P, 2, 2 * P], F32, name="sums")
+            for half in range(2):
+                values = slice(half * P, (half + 1) * P)
+                nc.tensor.matmul_mx(
+                    out=bank[:, half, :],
+                    lhsT=v_codes[:, values].bitcast(FP8X4),
+                    lhsT_scale=v_scales[:, values],
+                    rhs=codes[k][:, g, 2 * h : 2 * h + 2, :].rearrange("p r i -> p (r i)").bitcast(FP8X4),
+                    rhs_scale=scales[k][:, g, 2 * h : 2 * h + 2, :].rearrange("p r i -> p (r i)"),
+                    start=True,
+                    stop=True,
+                )
+            scaled[k, s] = scaled_sums.tile([P, 2, 2, P], F32, name="scaled")
+            nc.scalar.mul(
+                scaled[k, s][:].rearrange("v half e i -> v (half e i)"), bank[:].rearrange("v half c -> v (half c)"), SCALE
+            )
+
+        def add_to_state_on_tensor(k, s):
+            bank = sums_psum.tile([P, 2, 2, P], F32, name="sums")
+            state_quarters = state_bank[k, s].rearrange("i (e half v) -> i e half v", e=2, half=2)
+            for e in range(2):
+                for half in range(2):
+                    nc.tensor.matmul(
+                        out=bank[:, e, half, :], lhsT=scaled[k, s][:, half, e, :], rhs=identity[:], is_transpose=True, start=True, stop=False
+                    )
+                    nc.tensor.matmul(
+                        out=bank[:, e, half, :], lhsT=identity_bf16[:], rhs=state_quarters[:, e, half, :], start=False, stop=True
+                    )
+            nc.scalar.copy(out=new_state[k, s // 2][:, s % 2, :], in_=bank[:].rearrange("i e half v -> i (e half v)"))
+
         def multiply(k, g):
             for h in range(2):
                 s = 2 * g + h
+                if (k, s) in TENSOR_ADDS:
+                    multiply_turned(k, s)
+                    continue
                 sums[k, s] = sums_psum.tile([P, 2, VALUES], F32, name="sums")
                 for e in range(2):
                     nc.tensor.matmul_mx(
@@ -237,6 +275,8 @@ def tile_attention_pb_kernel(tc, Q, V, state, cos, sin, out):
             new_state[k, pair] = results.tile([P, 2, 2 * VALUES], F32, name="new_state")
             for h in range(2):
                 s = 2 * pair + h
+                if (k, s) in TENSOR_ADDS:
+                    continue
                 nc.vector.scalar_tensor_tensor(
                     out=new_state[k, pair][:, h, :],
                     in0=sums[k, s][:].rearrange("i e d -> i (e d)"),
@@ -273,7 +313,7 @@ def tile_attention_pb_kernel(tc, Q, V, state, cos, sin, out):
         last_load = max(load_turn)
         for k in range(CHUNKS):
             for pair in range(2):
-                added = TURNED * k + pair + (4 if k == LAST else 5)
+                added = TURNED * k + pair + (4 if k == LAST else 5) + ((k, 2 * pair + 1) in TENSOR_ADDS)
                 latest = added + TURNED * RESULT_BUFS // 2 - STORE_TURNS
                 store_turn.setdefault(min(latest, max(added + 1, last_load)), []).append((k, pair))
 
@@ -300,6 +340,8 @@ def tile_attention_pb_kernel(tc, Q, V, state, cos, sin, out):
                     add_rope(unit_of_turn(turn - 1))
                 if chunk_due(turn, 5, 4) is not None:
                     multiply(chunk_due(turn, 5, 4), 0)
+                if (chunk_due(turn, 7, 6), 3) in TENSOR_ADDS:
+                    add_to_state_on_tensor(chunk_due(turn, 7, 6), 3)
                 if chunk_due(turn, 6, 5) is not None:
                     multiply(chunk_due(turn, 6, 5), 1)
                 if within(turn + 1):

@@ -144,22 +144,15 @@ def tile_attention_pb_kernel(tc, Q, V, state, cos, sin, out):
         def turn_q(u):
             bank = q_psum.tile([P, PACK, P], F32, name="q_bank")
             turn_words(bank, q_unit[u])
-            q_turned[u] = turned_q.tile([P, 2, 2 * PACK * P], BF16, name="q_turned")
-            nc.scalar.copy(out=q_turned[u][:, 1].bitcast(F32), in_=bank[:].rearrange("i j p -> i (j p)"))
-            nc.scalar.mul(
-                q_turned[u][:, 0].rearrange("i (n e) -> i e n", e=2)[:, 0],
-                bank[:].bitcast(BF16).rearrange("i j (p e) -> i e j p", e=2)[:, ODD].rearrange("i j p -> i (j p)"),
-                -1.0,
-            )
+            q_turned[u] = turned_q.tile([P, PACK, 2 * P], BF16, name="q_turned")
+            nc.scalar.copy(out=q_turned[u][:].bitcast(F32), in_=bank[:])
 
         def turn_table(turned, rows, u):
             turned[u] = table_psum.tile([P, PACK, P], F32, name="table_bank")
             turn_words(turned[u], rows[u])
 
         def multiply_rope(u):
-            pairs = q_turned[u][:].rearrange("i k (n e) -> i k e n", e=2)
-            q_halves = pairs[:, 1]
-            q_crossed = pairs[:, :, EVEN]
+            q_halves = by_half(q_turned[u][:])
             cos_halves = by_half(cos_turned[u][:].bitcast(BF16))
             sin_halves = by_half(sin_turned[u][:].bitcast(BF16))
             same[u] = products.tile([P, 2, PACK, P], F32, name="same")
@@ -167,8 +160,16 @@ def tile_attention_pb_kernel(tc, Q, V, state, cos, sin, out):
             nc.vector.tensor_tensor(
                 out=same[u][:].rearrange("i e j p -> i e (j p)"), in0=cos_halves, in1=q_halves, op=MULT
             )
+            nc.vector.scalar_tensor_tensor(
+                out=other[u][:, EVEN].rearrange("i j p -> i (j p)"),
+                in0=sin_halves[:, EVEN],
+                scalar=-1.0,
+                in1=q_halves[:, ODD],
+                op0=MULT,
+                op1=MULT,
+            )
             nc.vector.tensor_tensor(
-                out=other[u][:].rearrange("i e j p -> i e (j p)"), in0=sin_halves, in1=q_crossed, op=MULT
+                out=other[u][:, ODD].rearrange("i j p -> i (j p)"), in0=sin_halves[:, ODD], in1=q_halves[:, EVEN], op=MULT
             )
 
         def place_in_grouped(k, s, e):

@@ -184,13 +184,16 @@ def tile_attention_pb_kernel(tc, Q, V, state, cos, sin, out):
                 )
             for e in (EVEN, ODD):
                 bank = rope_psum.tile([P, PACK, P], F32, name="rope_bank")
-                for j in range(PACK):
-                    nc.tensor.matmul(
-                        out=bank[:, j, :], lhsT=same[u][:, e, j, :], rhs=identity[:], is_transpose=True, start=True, stop=False
-                    )
-                    nc.tensor.matmul(
-                        out=bank[:, j, :], lhsT=other[u][:, e, j, :], rhs=identity[:], is_transpose=True, start=False, stop=True
-                    )
+                for product, first, last in ((same, 0, None), (other, None, PACK - 1)):
+                    for j in range(PACK):
+                        nc.tensor.matmul(
+                            out=bank[:, j, :],
+                            lhsT=product[u][:, e, j, :],
+                            rhs=identity[:],
+                            is_transpose=True,
+                            start=j == first,
+                            stop=j == last,
+                        )
                 nc.scalar.copy(out=place_in_grouped(k, s, e), in_=by_parity(bank[:]))
 
         def rope_on_gpsimd(k):

@@ -39,6 +39,17 @@ LOAD_AHEAD = 6
 RESULT_BUFS = 10
 STORE_TURNS = 3
 FIRST_TURN = -2
+LATE_CHUNKS = 0
+Q_SHARED = False
+OTHER_FIRST = False
+MM_FIRST = True
+TABLE_BANKS = 3
+ROPE_BANKS = 2
+SUM_BANKS = 2
+ORDER = 'ABMQcCS'
+ONE_BURST = False
+M_TURN = 5
+M_LAST = 4
 TENSOR_ADDS = [(k, 3) for k in range(CHUNKS - 2)]
 
 FLOPS = 2 * TOKENS * FEATURES * VALUES
@@ -91,10 +102,10 @@ def tile_attention_pb_kernel(tc, Q, V, state, cos, sin, out):
         quantised = ctx.enter_context(tc.tile_pool(name="quantised", bufs=2))
         scaled_sums = ctx.enter_context(tc.tile_pool(name="scaled_sums", bufs=1))
         results = ctx.enter_context(tc.tile_pool(name="results", bufs=RESULT_BUFS))
-        q_psum = ctx.enter_context(tc.psum_pool(name="q_psum", bufs=1))
-        table_psum = ctx.enter_context(tc.psum_pool(name="table_psum", bufs=3))
-        rope_psum = ctx.enter_context(tc.psum_pool(name="rope_psum", bufs=2))
-        sums_psum = ctx.enter_context(tc.psum_pool(name="sums_psum", bufs=2))
+        q_psum = ctx.enter_context(tc.psum_pool(name="q_psum", bufs=1)) if not Q_SHARED else None
+        table_psum = ctx.enter_context(tc.psum_pool(name="table_psum", bufs=TABLE_BANKS))
+        rope_psum = ctx.enter_context(tc.psum_pool(name="rope_psum", bufs=ROPE_BANKS))
+        sums_psum = ctx.enter_context(tc.psum_pool(name="sums_psum", bufs=SUM_BANKS))
 
         identity = keep.tile([P, P], F32)
         make_identity(nc, identity[:])
@@ -113,7 +124,7 @@ def tile_attention_pb_kernel(tc, Q, V, state, cos, sin, out):
             in_=v_grouped[:].rearrange("p d j -> p (d j)"),
         )
 
-        q_unit, cos_unit, sin_unit, state_bank = {}, {}, {}, {}
+        q_unit, cos_unit, sin_unit, state_bank, q_bank = {}, {}, {}, {}, {}
         q_turned, cos_turned, sin_turned, same, other = {}, {}, {}, {}, {}
         rotated, grouped, codes, scales, sums, new_state, scaled = {}, {}, {}, {}, {}, {}, {}
 
@@ -142,10 +153,13 @@ def tile_attention_pb_kernel(tc, Q, V, state, cos, sin, out):
                 nc.tensor.transpose(out=bank[:, j, :], in_=rows[:, j, :].bitcast(F32), identity=identity[:])
 
         def turn_q(u):
-            bank = q_psum.tile([P, PACK, P], F32, name="q_bank")
+            bank = (rope_psum if Q_SHARED else q_psum).tile([P, PACK, P], F32, name="rope_bank" if Q_SHARED else "q_bank")
             turn_words(bank, q_unit[u])
+            q_bank[u] = bank
+
+        def copy_q(u):
             q_turned[u] = turned_q.tile([P, PACK, 2 * P], BF16, name="q_turned")
-            nc.scalar.copy(out=q_turned[u][:].bitcast(F32), in_=bank[:])
+            nc.scalar.copy(out=q_turned[u][:].bitcast(F32), in_=q_bank[u][:])
 
         def turn_table(turned, rows, u):
             turned[u] = table_psum.tile([P, PACK, P], F32, name="table_bank")
@@ -176,15 +190,15 @@ def tile_attention_pb_kernel(tc, Q, V, state, cos, sin, out):
             g, half = divmod(s, GROUP)
             return grouped[k][:, g, e::2, half * (P // 2) : (half + 1) * (P // 2), :]
 
-        def add_rope(u):
+        def add_rope(u, halves_now):
             k, s = divmod(u, CHUNK)
-            if s == 0:
+            if s == 0 and k not in grouped:
                 grouped[k] = turnstile.tile(
                     [P, GROUPS, ROWS, P, PACK], BF16, name="grouped%d" % (k % 3), offset=(k % 3) * GROUPED_BYTES, align_bytes=64
                 )
-            for e in (EVEN, ODD):
+            for e in halves_now:
                 bank = rope_psum.tile([P, PACK, P], F32, name="rope_bank")
-                for product, first, last in ((same, 0, None), (other, None, PACK - 1)):
+                for product, first, last in (((other, 0, None), (same, None, PACK - 1)) if OTHER_FIRST else ((same, 0, None), (other, None, PACK - 1))):
                     for j in range(PACK):
                         nc.tensor.matmul(
                             out=bank[:, j, :],
@@ -246,15 +260,21 @@ def tile_attention_pb_kernel(tc, Q, V, state, cos, sin, out):
 
         def add_to_state_on_tensor(k, s):
             bank = sums_psum.tile([P, 2, 2, P], F32, name="sums")
-            state_quarters = state_bank[k, s].rearrange("i (e half v) -> i e half v", e=2, half=2)
+            columns = bank[:].rearrange("i e half v -> i (e half v)")
+            if MM_FIRST:
+                nc.tensor.matmul(out=columns, lhsT=identity_bf16[:], rhs=state_bank[k, s], start=True, stop=False)
             for e in range(2):
                 for half in range(2):
                     nc.tensor.matmul(
-                        out=bank[:, e, half, :], lhsT=scaled[k, s][:, half, e, :], rhs=identity[:], is_transpose=True, start=True, stop=False
+                        out=bank[:, e, half, :],
+                        lhsT=scaled[k, s][:, half, e, :],
+                        rhs=identity[:],
+                        is_transpose=True,
+                        start=(e, half) == (0, 0) and not MM_FIRST,
+                        stop=(e, half) == (1, 1) and MM_FIRST,
                     )
-                    nc.tensor.matmul(
-                        out=bank[:, e, half, :], lhsT=identity_bf16[:], rhs=state_quarters[:, e, half, :], start=False, stop=True
-                    )
+            if not MM_FIRST:
+                nc.tensor.matmul(out=columns, lhsT=identity_bf16[:], rhs=state_bank[k, s], start=False, stop=True)
             nc.scalar.copy(out=new_state[k, s // 2][:, s % 2, :], in_=bank[:].rearrange("i e half v -> i (e half v)"))
 
         def multiply(k, g):
@@ -312,12 +332,16 @@ def tile_attention_pb_kernel(tc, Q, V, state, cos, sin, out):
             load_turn.setdefault(at, []).append(n)
 
         LAST = CHUNKS - 1
+        g0_turn = [TURNED * k + (M_LAST if k == LAST else M_TURN) for k in range(CHUNKS)]
+        g1_turn = [t + (0 if ONE_BURST and k < LAST else 1) for k, t in enumerate(g0_turn)]
+        a1_turn = [t + 1 for t in g0_turn]
+        f_turn = [t + 1 for t in a1_turn]
 
         store_turn = {}
         last_load = max(load_turn)
         for k in range(CHUNKS):
             for pair in range(2):
-                added = TURNED * k + pair + (4 if k == LAST else 5) + ((k, 2 * pair + 1) in TENSOR_ADDS)
+                added = (g0_turn, a1_turn)[pair][k] + ((k, 2 * pair + 1) in TENSOR_ADDS)
                 latest = added + TURNED * RESULT_BUFS // 2 - STORE_TURNS
                 store_turn.setdefault(min(latest, max(added + 1, last_load)), []).append((k, pair))
 
@@ -337,24 +361,34 @@ def tile_attention_pb_kernel(tc, Q, V, state, cos, sin, out):
                 if chunk_due(turn, -1, -1) is not None:
                     load_state(chunk_due(turn, -1, -1))
                 for k, pair in store_turn.get(turn, []):
-                    store(k, pair, 2 if (k, pair) == (LAST, 1) else 1)
+                    store(k, pair, 2 if k == LAST else 1)
                 if chunk_due(turn, 3, 3) is not None:
                     regroup(chunk_due(turn, 3, 3))
-                if within(turn - 1):
-                    add_rope(unit_of_turn(turn - 1))
-                if chunk_due(turn, 5, 4) is not None:
-                    multiply(chunk_due(turn, 5, 4), 0)
-                if (chunk_due(turn, 7, 6), 3) in TENSOR_ADDS:
-                    add_to_state_on_tensor(chunk_due(turn, 7, 6), 3)
-                if chunk_due(turn, 6, 5) is not None:
-                    multiply(chunk_due(turn, 6, 5), 1)
-                if within(turn + 1):
-                    turn_table(cos_turned, cos_unit, unit_of_turn(turn + 1))
-                if within(turn + 2):
-                    turn_q(unit_of_turn(turn + 2))
-                if within(turn + 1):
-                    turn_table(sin_turned, sin_unit, unit_of_turn(turn + 1))
-                if within(turn):
+                for step in ORDER:
+                    if step == 'A' and within(turn - 1):
+                        add_rope(unit_of_turn(turn - 1), (EVEN,))
+                    if step == 'B' and within(turn - 1):
+                        add_rope(unit_of_turn(turn - 1), (ODD,))
+                    if step == 'M':
+                        for k in range(CHUNKS):
+                            if turn == f_turn[k] and (k, 3) in TENSOR_ADDS:
+                                add_to_state_on_tensor(k, 3)
+                        for k in range(CHUNKS):
+                            if turn == g0_turn[k]:
+                                multiply(k, 0)
+                            if turn == g1_turn[k]:
+                                multiply(k, 1)
+                    if step == 'c' and within(turn + 2):
+                        copy_q(unit_of_turn(turn + 2))
+                    if step == 'C' and within(turn + 1):
+                        turn_table(cos_turned, cos_unit, unit_of_turn(turn + 1))
+                    if step == 'Q' and within(turn + 2):
+                        turn_q(unit_of_turn(turn + 2))
+                    if step == 'S' and within(turn + 1):
+                        turn_table(sin_turned, sin_unit, unit_of_turn(turn + 1))
+                    if step == 'P' and within(turn):
+                        multiply_rope(unit_of_turn(turn))
+                if within(turn) and 'P' not in ORDER:
                     multiply_rope(unit_of_turn(turn))
                 if turn == TURNED * LAST + 3:
                     quantise(LAST, 0, 1)
@@ -364,7 +398,8 @@ def tile_attention_pb_kernel(tc, Q, V, state, cos, sin, out):
                     quantise(chunk_due(turn, 4, 4), 0, GROUPS)
                 if chunk_due(turn, -2, -2) is not None:
                     rope_on_gpsimd(chunk_due(turn, -2, -2))
-                if chunk_due(turn, 5, 4) is not None:
-                    add_to_state(chunk_due(turn, 5, 4), 0)
-                if chunk_due(turn, 6, 5) is not None:
-                    add_to_state(chunk_due(turn, 6, 5), 1)
+                for k in range(CHUNKS):
+                    if turn == g0_turn[k]:
+                        add_to_state(k, 0)
+                    if turn == a1_turn[k]:
+                        add_to_state(k, 1)

@@ -36,7 +36,7 @@ assert sum(LOAD_UNITS) == UNITS
 LOAD_BUFS = 4
 STATE_BUFS = 4
 LOAD_AHEAD = 6
-RESULT_BUFS = 10
+RESULT_BUFS = 12
 STORE_TURNS = 3
 FIRST_TURN = -2
 LATE_CHUNKS = 0

from contextlib import ExitStack

import concourse.mybir as mybir
from concourse.masks import make_identity

F32 = mybir.dt.float32
BF16 = mybir.dt.bfloat16
U32 = mybir.dt.uint32
U8 = mybir.dt.uint8
FP8X4 = mybir.dt.float8_e4m3fn_x4
MULT = mybir.AluOpType.mult
ADD = mybir.AluOpType.add
SUBTRACT = mybir.AluOpType.subtract

P = 128
PACK = 4
TOKENS = P * PACK
FEATURES = 8192
VALUES = 256
SCALE = FEATURES**-0.5

UNIT = 2 * P
UNITS = FEATURES // UNIT
CHUNK = 4
CHUNKS = UNITS // CHUNK
TURNED = CHUNK - 1
TURNS = CHUNKS * TURNED
EVEN, ODD = 0, 1
GROUP = 2
GROUPS = CHUNK // GROUP
ROWS = 2 * GROUP
BANKS = CHUNK
GROUPED_BYTES = CHUNK * UNIT * PACK * 2
LOAD_UNITS = (CHUNK,) * CHUNKS
assert sum(LOAD_UNITS) == UNITS
LOAD_BUFS = 4
STATE_BUFS = 4
LOAD_AHEAD = 6
RESULT_BUFS = 12
STORE_TURNS = 3
FIRST_TURN = -2
LATE_CHUNKS = 0
Q_SHARED = False
OTHER_FIRST = False
MM_FIRST = True
TABLE_BANKS = 3
ROPE_BANKS = 2
SUM_BANKS = 2
ORDER = 'ABMQcCS'
ONE_BURST = False
M_TURN = 5
M_LAST = 4
TENSOR_ADDS = [(k, 3) for k in range(CHUNKS - 2)]

FLOPS = 2 * TOKENS * FEATURES * VALUES


def unit_of_turn(v):
    return CHUNK * (v // TURNED) + v % TURNED


def first_use(u):
    k, s = divmod(u, CHUNK)
    return TURNED * k - 2 if s == TURNED else TURNED * k + s - 2


def last_use(u):
    k, s = divmod(u, CHUNK)
    return TURNED * k - 2 if s == TURNED else TURNED * k + s - 1


def halves(rows):
    return rows.rearrange("p j (i e) -> p e j i", e=2)


def by_half(turned):
    return turned.rearrange("i j (p e) -> i e (j p)", e=2)


def by_parity(sums):
    return sums.rearrange("p j (m parity) -> p parity m j", parity=2)


def tile_attention_pb_kernel(tc, Q, V, state, cos, sin, out):
    nc = tc.nc

    q_rows = Q.flatten_outer_dims().rearrange("(p j) f -> p j f", j=PACK)
    cos_rows = cos.rearrange("(p j) f -> p j f", j=PACK)
    sin_rows = sin.rearrange("(p j) f -> p j f", j=PACK)
    v_rows = V.flatten_outer_dims().rearrange("(p j) d -> p j d", j=PACK)
    state_rows = state.flatten_outer_dims().rearrange("(n i r) d -> i n (r d)", i=P, r=ROWS)
    out_rows = out.flatten_outer_dims().rearrange("(n i r) d -> i n (r d)", i=P, r=ROWS)

    with ExitStack() as ctx:
        keep = ctx.enter_context(tc.tile_pool(name="keep", bufs=1))
        loads = ctx.enter_context(tc.tile_pool(name="loads", bufs=LOAD_BUFS))
        states = ctx.enter_context(tc.tile_pool(name="states", bufs=STATE_BUFS))
        turned_q = ctx.enter_context(tc.tile_pool(name="turned_q", bufs=3))
        products = ctx.enter_context(tc.tile_pool(name="products", bufs=2))
        turnstile = ctx.enter_context(tc.tile_pool(name="turnstile", bufs=1))
        gpsimd_work = ctx.enter_context(tc.tile_pool(name="gpsimd_work", bufs=2))
        quantised = ctx.enter_context(tc.tile_pool(name="quantised", bufs=2))
        scaled_sums = ctx.enter_context(tc.tile_pool(name="scaled_sums", bufs=1))
        results = ctx.enter_context(tc.tile_pool(name="results", bufs=RESULT_BUFS))
        q_psum = ctx.enter_context(tc.psum_pool(name="q_psum", bufs=1)) if not Q_SHARED else None
        table_psum = ctx.enter_context(tc.psum_pool(name="table_psum", bufs=TABLE_BANKS))
        rope_psum = ctx.enter_context(tc.psum_pool(name="rope_psum", bufs=ROPE_BANKS))
        sums_psum = ctx.enter_context(tc.psum_pool(name="sums_psum", bufs=SUM_BANKS))

        identity = keep.tile([P, P], F32)
        make_identity(nc, identity[:])
        identity_bf16 = keep.tile([P, P], BF16)
        make_identity(nc, identity_bf16[:])

        v_raw = keep.tile([P, PACK, VALUES], BF16)
        nc.scalar.dma_start(out=v_raw[:], in_=v_rows)
        v_grouped = keep.tile([P, VALUES, PACK], BF16, align_bytes=64)
        nc.vector.tensor_copy(out=v_grouped[:], in_=v_raw[:].rearrange("p j d -> p d j"))
        v_codes = keep.tile([P, VALUES], U32, align_bytes=64)
        v_scales = keep.tile([P, VALUES], U8, align_bytes=64)
        nc.vector.quantize_mx(
            out=v_codes[:].bitcast(FP8X4),
            scales=v_scales[:],
            in_=v_grouped[:].rearrange("p d j -> p (d j)"),
        )

        q_unit, cos_unit, sin_unit, state_bank, q_bank = {}, {}, {}, {}, {}
        q_turned, cos_turned, sin_turned, same, other = {}, {}, {}, {}, {}
        rotated, grouped, codes, scales, sums, new_state, scaled = {}, {}, {}, {}, {}, {}, {}

        def load(first, units):
            features = slice(first * UNIT, (first + units) * UNIT)
            q_sb = loads.tile([P, PACK, units * UNIT], BF16)
            nc.sync.dma_start(out=q_sb[:], in_=q_rows[:, :, features])
            cos_sb = loads.tile([P, PACK, units * UNIT], BF16)
            nc.sync.dma_start(out=cos_sb[:], in_=cos_rows[:, :, features])
            sin_sb = loads.tile([P, PACK, units * UNIT], BF16)
            nc.sync.dma_start(out=sin_sb[:], in_=sin_rows[:, :, features])
            for h in range(units):
                columns = slice(h * UNIT, (h + 1) * UNIT)
                q_unit[first + h] = q_sb[:, :, columns]
                cos_unit[first + h] = cos_sb[:, :, columns]
                sin_unit[first + h] = sin_sb[:, :, columns]

        def load_state(k):
            state_sb = states.tile([P, GROUPS, ROWS * VALUES], BF16)
            nc.sync.dma_start(out=state_sb[:], in_=state_rows[:, GROUPS * k : GROUPS * (k + 1), :])
            for b in range(BANKS):
                state_bank[k, b] = state_sb[:].rearrange("i g (h c) -> i (g h) c", h=2)[:, b, :]

        def turn_words(bank, rows):
            for j in range(PACK):
                nc.tensor.transpose(out=bank[:, j, :], in_=rows[:, j, :].bitcast(F32), identity=identity[:])

        def turn_q(u):
            bank = (rope_psum if Q_SHARED else q_psum).tile([P, PACK, P], F32, name="rope_bank" if Q_SHARED else "q_bank")
            turn_words(bank, q_unit[u])
            q_bank[u] = bank

        def copy_q(u):
            q_turned[u] = turned_q.tile([P, PACK, 2 * P], BF16, name="q_turned")
            nc.scalar.copy(out=q_turned[u][:].bitcast(F32), in_=q_bank[u][:])

        def turn_table(turned, rows, u):
            turned[u] = table_psum.tile([P, PACK, P], F32, name="table_bank")
            turn_words(turned[u], rows[u])

        def multiply_rope(u):
            q_halves = by_half(q_turned[u][:])
            cos_halves = by_half(cos_turned[u][:].bitcast(BF16))
            sin_halves = by_half(sin_turned[u][:].bitcast(BF16))
            same[u] = products.tile([P, 2, PACK, P], F32, name="same")
            other[u] = products.tile([P, 2, PACK, P], F32, name="other")
            nc.vector.tensor_tensor(
                out=same[u][:].rearrange("i e j p -> i e (j p)"), in0=cos_halves, in1=q_halves, op=MULT
            )
            nc.vector.scalar_tensor_tensor(
                out=other[u][:, EVEN].rearrange("i j p -> i (j p)"),
                in0=sin_halves[:, EVEN],
                scalar=-1.0,
                in1=q_halves[:, ODD],
                op0=MULT,
                op1=MULT,
            )
            nc.vector.tensor_tensor(
                out=other[u][:, ODD].rearrange("i j p -> i (j p)"), in0=sin_halves[:, ODD], in1=q_halves[:, EVEN], op=MULT
            )

        def place_in_grouped(k, s, e):
            g, half = divmod(s, GROUP)
            return grouped[k][:, g, e::2, half * (P // 2) : (half + 1) * (P // 2), :]

        def add_rope(u, halves_now):
            k, s = divmod(u, CHUNK)
            if s == 0 and k not in grouped:
                grouped[k] = turnstile.tile(
                    [P, GROUPS, ROWS, P, PACK], BF16, name="grouped%d" % (k % 3), offset=(k % 3) * GROUPED_BYTES, align_bytes=64
                )
            for e in halves_now:
                bank = rope_psum.tile([P, PACK, P], F32, name="rope_bank")
                for product, first, last in (((other, 0, None), (same, None, PACK - 1)) if OTHER_FIRST else ((same, 0, None), (other, None, PACK - 1))):
                    for j in range(PACK):
                        nc.tensor.matmul(
                            out=bank[:, j, :],
                            lhsT=product[u][:, e, j, :],
                            rhs=identity[:],
                            is_transpose=True,
                            start=j == first,
                            stop=j == last,
                        )
                nc.scalar.copy(out=place_in_grouped(k, s, e), in_=by_parity(bank[:]))

        def rope_on_gpsimd(k):
            u = CHUNK * k + TURNED
            q_halves = halves(q_unit[u])
            place = (k - 2) % 3
            first = turnstile.tile(
                [P, 2, PACK, P], F32, name="gpsimd_same%d" % place, offset=place * GROUPED_BYTES, align_bytes=64
            )
            second = gpsimd_work.tile([P, 2, PACK, P], F32, name="gpsimd_other", bufs=1)
            rotated[k] = gpsimd_work.tile([P, 2, PACK, P], F32, name="rotated")
            nc.gpsimd.tensor_tensor(out=first[:], in0=halves(cos_unit[u]), in1=q_halves, op=MULT)
            nc.gpsimd.tensor_tensor(out=second[:], in0=halves(sin_unit[u]), in1=q_halves[:, ::-1], op=MULT)
            for e, combine in ((EVEN, SUBTRACT), (ODD, ADD)):
                nc.gpsimd.tensor_tensor(out=rotated[k][:, e], in0=first[:, e], in1=second[:, e], op=combine)

        def regroup(k):
            for e in (EVEN, ODD):
                nc.scalar.copy(out=place_in_grouped(k, TURNED, e), in_=by_parity(rotated[k][:, e]))

        def quantise(k, first, groups):
            if first == 0:
                codes[k] = quantised.tile([P, GROUPS, ROWS, P], U32, align_bytes=64, name="codes")
                scales[k] = quantised.tile([P, GROUPS, ROWS, P], U8, align_bytes=64, name="scales")
            part = slice(first, first + groups)
            nc.vector.quantize_mx(
                out=codes[k][:, part].rearrange("p g r i -> p (g r i)").bitcast(FP8X4),
                scales=scales[k][:, part].rearrange("p g r i -> p (g r i)"),
                in_=grouped[k][:, part].rearrange("p g r i j -> p (g r i j)"),
            )

        def multiply_turned(k, s):
            g, h = divmod(s, 2)
            bank = sums_psum.tile([P, 2, 2 * P], F32, name="sums")
            for half in range(2):
                values = slice(half * P, (half + 1) * P)
                nc.tensor.matmul_mx(
                    out=bank[:, half, :],
                    lhsT=v_codes[:, values].bitcast(FP8X4),
                    lhsT_scale=v_scales[:, values],
                    rhs=codes[k][:, g, 2 * h : 2 * h + 2, :].rearrange("p r i -> p (r i)").bitcast(FP8X4),
                    rhs_scale=scales[k][:, g, 2 * h : 2 * h + 2, :].rearrange("p r i -> p (r i)"),
                    start=True,
                    stop=True,
                )
            scaled[k, s] = scaled_sums.tile([P, 2, 2, P], F32, name="scaled")
            nc.scalar.mul(
                scaled[k, s][:].rearrange("v half e i -> v (half e i)"), bank[:].rearrange("v half c -> v (half c)"), SCALE
            )

        def add_to_state_on_tensor(k, s):
            bank = sums_psum.tile([P, 2, 2, P], F32, name="sums")
            columns = bank[:].rearrange("i e half v -> i (e half v)")
            if MM_FIRST:
                nc.tensor.matmul(out=columns, lhsT=identity_bf16[:], rhs=state_bank[k, s], start=True, stop=False)
            for e in range(2):
                for half in range(2):
                    nc.tensor.matmul(
                        out=bank[:, e, half, :],
                        lhsT=scaled[k, s][:, half, e, :],
                        rhs=identity[:],
                        is_transpose=True,
                        start=(e, half) == (0, 0) and not MM_FIRST,
                        stop=(e, half) == (1, 1) and MM_FIRST,
                    )
            if not MM_FIRST:
                nc.tensor.matmul(out=columns, lhsT=identity_bf16[:], rhs=state_bank[k, s], start=False, stop=True)
            nc.scalar.copy(out=new_state[k, s // 2][:, s % 2, :], in_=bank[:].rearrange("i e half v -> i (e half v)"))

        def multiply(k, g):
            for h in range(2):
                s = 2 * g + h
                if (k, s) in TENSOR_ADDS:
                    multiply_turned(k, s)
                    continue
                sums[k, s] = sums_psum.tile([P, 2, VALUES], F32, name="sums")
                for e in range(2):
                    nc.tensor.matmul_mx(
                        out=sums[k, s][:, e, :],
                        lhsT=codes[k][:, g, 2 * h + e, :].bitcast(FP8X4),
                        lhsT_scale=scales[k][:, g, 2 * h + e, :],
                        rhs=v_codes[:].bitcast(FP8X4),
                        rhs_scale=v_scales[:],
                        start=True,
                        stop=True,
                    )

        def add_to_state(k, pair):
            new_state[k, pair] = results.tile([P, 2, 2 * VALUES], F32, name="new_state")
            for h in range(2):
                s = 2 * pair + h
                if (k, s) in TENSOR_ADDS:
                    continue
                nc.vector.scalar_tensor_tensor(
                    out=new_state[k, pair][:, h, :],
                    in0=sums[k, s][:].rearrange("i e d -> i (e d)"),
                    scalar=SCALE,
                    in1=state_bank[k, s],
                    op0=MULT,
                    op1=ADD,
                )

        def store(k, pair, pieces):
            width = ROWS * VALUES // pieces
            for n in range(pieces):
                columns = slice(n * width, (n + 1) * width)
                nc.sync.dma_start(
                    out=out_rows[:, GROUPS * k + pair, columns],
                    in_=new_state[k, pair][:].rearrange("i h c -> i (h c)")[:, columns],
                )

        load_turn = {}
        firsts = [sum(LOAD_UNITS[:n]) for n in range(len(LOAD_UNITS))]

        def units_of_load(n):
            return range(firsts[n], firsts[n] + LOAD_UNITS[n])

        for n in range(len(LOAD_UNITS)):
            at = max(FIRST_TURN, min([first_use(u) for u in units_of_load(n)]) - LOAD_AHEAD)
            if n >= LOAD_BUFS:
                at = max(at, max([last_use(u) for u in units_of_load(n - LOAD_BUFS)]) + 1)
            load_turn.setdefault(at, []).append(n)

        LAST = CHUNKS - 1
        g0_turn = [TURNED * k + (M_LAST if k == LAST else M_TURN) for k in range(CHUNKS)]
        g1_turn = [t + (0 if ONE_BURST and k < LAST else 1) for k, t in enumerate(g0_turn)]
        a1_turn = [t + 1 for t in g0_turn]
        f_turn = [t + 1 for t in a1_turn]

        store_turn = {}
        last_load = max(load_turn)
        for k in range(CHUNKS):
            for pair in range(2):
                added = (g0_turn, a1_turn)[pair][k] + ((k, 2 * pair + 1) in TENSOR_ADDS)
                latest = added + TURNED * RESULT_BUFS // 2 - STORE_TURNS
                store_turn.setdefault(min(latest, max(added + 1, last_load)), []).append((k, pair))

        def chunk_due(turn, delay, last_delay):
            if turn - last_delay == TURNED * LAST:
                return LAST
            k, rest = divmod(turn - delay, TURNED)
            return k if rest == 0 and 0 <= k < LAST else None

        def within(v):
            return 0 <= v < TURNS

        with tc.manual_schedule():
            for turn in range(FIRST_TURN, TURNS + 4):
                for n in load_turn.get(turn, []):
                    load(firsts[n], LOAD_UNITS[n])
                if chunk_due(turn, -1, -1) is not None:
                    load_state(chunk_due(turn, -1, -1))
                for k, pair in store_turn.get(turn, []):
                    store(k, pair, 2 if k == LAST else 1)
                if chunk_due(turn, 3, 3) is not None:
                    regroup(chunk_due(turn, 3, 3))
                for step in ORDER:
                    if step == 'A' and within(turn - 1):
                        add_rope(unit_of_turn(turn - 1), (EVEN,))
                    if step == 'B' and within(turn - 1):
                        add_rope(unit_of_turn(turn - 1), (ODD,))
                    if step == 'M':
                        for k in range(CHUNKS):
                            if turn == f_turn[k] and (k, 3) in TENSOR_ADDS:
                                add_to_state_on_tensor(k, 3)
                        for k in range(CHUNKS):
                            if turn == g0_turn[k]:
                                multiply(k, 0)
                            if turn == g1_turn[k]:
                                multiply(k, 1)
                    if step == 'c' and within(turn + 2):
                        copy_q(unit_of_turn(turn + 2))
                    if step == 'C' and within(turn + 1):
                        turn_table(cos_turned, cos_unit, unit_of_turn(turn + 1))
                    if step == 'Q' and within(turn + 2):
                        turn_q(unit_of_turn(turn + 2))
                    if step == 'S' and within(turn + 1):
                        turn_table(sin_turned, sin_unit, unit_of_turn(turn + 1))
                    if step == 'P' and within(turn):
                        multiply_rope(unit_of_turn(turn))
                if within(turn) and 'P' not in ORDER:
                    multiply_rope(unit_of_turn(turn))
                if turn == TURNED * LAST + 3:
                    quantise(LAST, 0, 1)
                elif turn == TURNED * LAST + 4:
                    quantise(LAST, 1, 1)
                elif chunk_due(turn, 4, 4) is not None:
                    quantise(chunk_due(turn, 4, 4), 0, GROUPS)
                if chunk_due(turn, -2, -2) is not None:
                    rope_on_gpsimd(chunk_due(turn, -2, -2))
                for k in range(CHUNKS):
                    if turn == g0_turn[k]:
                        add_to_state(k, 0)
                    if turn == a1_turn[k]:
                        add_to_state(k, 1)
